import numpy as np
import ml_dtypes


def mxq(x, axis, fmt="e4m3"):
    dtype, down = {"e4m3": (ml_dtypes.float8_e4m3fn, 7), "e5m2": (ml_dtypes.float8_e5m2, 14)}[fmt]
    v = np.moveaxis(np.asarray(x, np.float32).astype(ml_dtypes.bfloat16).astype(np.float64), axis, -1)
    blocks = v.reshape(v.shape[:-1] + (-1, 32))
    amax = np.abs(blocks).max(-1, keepdims=True)
    byte = np.maximum(np.where(amax > 0, np.frexp(amax)[1] - 1 + 127, 0) - down, 1)
    scale = np.exp2(byte - 127.0)
    codes = (blocks / scale).astype(np.float32).astype(dtype).astype(np.float64)
    return np.moveaxis((codes * scale).reshape(v.shape), -1, axis)


WIDE = False


def mx_kscale(k):
    if not WIDE:
        return np.ones(k)
    levels = np.array([10, -10, 5, -5, 0])
    if k % 512:
        return np.exp2(np.random.permutation(np.resize(levels, k // 32))).repeat(32)
    a = np.empty((k // 512, 16))
    for p in range(k // 512):
        a[p, :8] = np.random.permutation(np.resize(levels, 8))
        for g in range(8):
            far = levels[np.abs(levels - a[p, g]) >= 10]
            a[p, g + 8] = far[np.random.randint(len(far))]
    return np.exp2(a.ravel()).repeat(32)


BF16 = ml_dtypes.bfloat16


def bf(x):
    return np.asarray(x, np.float32).astype(BF16)


def f64(x):
    return np.asarray(x).astype(np.float64)


B, L, EMB, HD, NH = 2, 512, 1024, 128, 16
THETA = 10000.0


def rope_mats(seq_len):
    freqs = 1.0 / THETA ** (f64(np.arange(0, HD, 2)) / HD)
    t = f64(np.arange(seq_len))
    f = np.repeat(t[:, None] * freqs[None, :], 2, axis=-1)
    return np.cos(f), np.sin(f)


def apply_rope(u, rc, rs):
    ue = u[..., 0::2]
    uo = u[..., 1::2]
    u_rot = np.stack([-uo, ue], axis=-1).reshape(u.shape)
    return u * rc + u_rot * rs


def draw0():
    s = mx_kscale(EMB)
    w = 1.0 / np.sqrt(EMB)
    return {"x": bf(np.random.standard_normal((B, L, EMB)) * s),
            "Wq": bf(np.random.standard_normal((EMB, HD * NH)) * w / s[:, None]),
            "Wk": bf(np.random.standard_normal((EMB, HD)) * w / s[:, None]),
            "Wv": bf(np.random.standard_normal((EMB, HD)) * w / s[:, None])}


def core(x, Wq, Wk, Wv):
    xq = mxq(f64(x), 2, "e4m3")
    Q = (xq @ mxq(f64(Wq), 0, "e4m3")).reshape(B, L, NH, HD).transpose(0, 2, 1, 3)
    K = xq @ mxq(f64(Wk), 0, "e4m3")
    V = xq @ mxq(f64(Wv), 0, "e4m3")
    rc, rs = rope_mats(L)
    return apply_rope(Q, rc, rs), apply_rope(K, rc, rs), V


def e4m3fn_bytes(y):
    return np.clip(np.asarray(y, np.float64), -448.0, 448.0).astype(np.float32).astype(ml_dtypes.float8_e4m3fn).view(np.uint8)


def e4m3fn_values(b):
    return np.asarray(b, np.uint8).view(ml_dtypes.float8_e4m3fn).astype(np.float64)


def setup_inputs():
    d = draw0()
    x0 = np.asarray(d['Wq']).astype(np.float64)
    s = (np.max(np.abs(x0), axis=(1,), keepdims=True) / 448.0).astype(np.float32)
    out = {}
    for k, v in d.items():
        if k == 'Wq':
            out['Wq_bytes'] = e4m3fn_bytes(x0 / s.astype(np.float64))
            out['Wq_scale'] = s
        else:
            out[k] = v
    return out


def reference(x, Wq_bytes, Wq_scale, Wk, Wv):
    return core(x, e4m3fn_values(Wq_bytes) * Wq_scale.astype(np.float64), Wk, Wv)

@@ -1,0 +1,291 @@
+import math
+from contextlib import ExitStack
+
+import concourse.mybir as mybir
+from concourse.masks import make_identity
+
+B, L, EMB, HD, NH = 2, 512, 1024, 128, 16
+THETA = 10000.0
+FLOPS = 2 * B * L * EMB * (HD * NH + 2 * HD)
+
+F32 = mybir.dt.float32
+BF16 = mybir.dt.bfloat16
+I32 = mybir.dt.int32
+U32 = mybir.dt.uint32
+U8 = mybir.dt.uint8
+FP8 = mybir.dt.float8_e4m3fn
+FP8X4 = mybir.dt.float8_e4m3fn_x4
+ALU = mybir.AluOpType
+ACT = mybir.ActivationFunctionType
+
+P = 128
+PACK = 4
+PASSES = EMB // (P * PACK)
+JT = L // P
+CH = 512
+NCH = HD * NH // CH
+HPC = CH // HD
+NK = HD // 2
+
+WIDEN = {(0, 1): "V"}
+INTER = {(0, 0): "G", (0, 1): "V"}
+XCOPY = {0: "S", 1: "S"}
+VADD = {(3, 1, 2), (3, 1, 3)}
+FINE_STORE = {(3, 1)}
+
+
+def tile_groupropeattention_pa_kernel(tc, x, Wq_bytes, Wq_scale, Wk, Wv, out_0, out_1, out_2):
+    nc = tc.nc
+    with ExitStack() as ctx:
+        keep = ctx.enter_context(tc.tile_pool(name="keep", bufs=1))
+        bytes_pool = ctx.enter_context(tc.tile_pool(name="bytes_pool", bufs=NCH * PASSES))
+        plane_pool = ctx.enter_context(tc.tile_pool(name="plane_pool", bufs=3))
+        group_pool = ctx.enter_context(tc.tile_pool(name="group_pool", bufs=3))
+        xg_pool = ctx.enter_context(tc.tile_pool(name="xg_pool", bufs=3))
+        prod_pool = ctx.enter_context(tc.tile_pool(name="prod_pool", bufs=3))
+        kv_pool = ctx.enter_context(tc.tile_pool(name="kv_pool", bufs=2))
+        psx = ctx.enter_context(tc.psum_pool(name="psx", bufs=2))
+        psa = ctx.enter_context(tc.psum_pool(name="psa", bufs=6))
+
+        pos = keep.tile([P, JT], F32)
+        nc.gpsimd.iota(pos[:], pattern=[[1, JT]], base=0, channel_multiplier=JT, allow_small_or_imprecise_dtypes=True)
+        zero1 = keep.tile([P, 1], F32)
+        nc.gpsimd.memset(zero1[:], 0.0)
+        warm = keep.tile([P, 1], F32)
+        nc.scalar.activation(out=warm[:], in_=zero1[:], func=ACT.Sin)
+        ident = keep.tile([P, P], F32)
+        make_identity(nc, ident[:])
+
+        wsc = keep.tile([P, PASSES, PACK], F32)
+        nc.sync.dma_start(out=wsc[:], in_=Wq_scale.rearrange("(g p t) o -> p g (t o)", p=P, t=PACK))
+        wq_view = Wq_bytes.rearrange("(g p t) n -> g p t n", p=P, t=PACK)
+        wbytes = {}
+
+        def load_wq(c):
+            for g in range(PASSES):
+                wq_codes_in = bytes_pool.tile([P, PACK, CH], U8)
+                nc.sync.dma_start(out=wq_codes_in[:], in_=wq_view[g][:, :, c * CH : (c + 1) * CH])
+                wbytes[(c, g)] = wq_codes_in
+
+        xr = {}
+
+        def load_x(b):
+            xv = x[b].rearrange("(p j) k -> p j k", j=JT)
+            for jh in range(2):
+                xraw = keep.tile([P, 2, EMB], BF16, name="xraw%d%d" % (b, jh))
+                nc.sync.dma_start(out=xraw[:], in_=xv[:, 2 * jh : 2 * jh + 2, :])
+                xr[(b, jh)] = xraw
+
+        load_wq(0)
+        load_x(0)
+        kvr = keep.tile([P, 2, PASSES, PACK, HD], BF16)
+        nc.sync.dma_start(
+            out=kvr[:, 0].rearrange("p g t n -> p g (t n)"), in_=Wk.rearrange("(g p t) n -> p g (t n)", p=P, t=PACK)
+        )
+        nc.sync.dma_start(
+            out=kvr[:, 1].rearrange("p g t n -> p g (t n)"), in_=Wv.rearrange("(g p t) n -> p g (t n)", p=P, t=PACK)
+        )
+        load_x(1)
+        for c in range(1, NCH):
+            load_wq(c)
+
+        NA = JT * NK
+        ang = keep.tile([P, JT, NK], F32)
+        nc.vector.tensor_copy(out=ang[:, :, 0:1], in_=pos[:].unsqueeze(2))
+        w = 1
+        while w < NK:
+            nc.vector.tensor_scalar(
+                out=ang[:, :, w : 2 * w], in0=ang[:, :, 0:w], scalar1=THETA ** (-2.0 * w / HD), scalar2=None, op0=ALU.mult
+            )
+            w *= 2
+        angf = ang[:].rearrange("p j k -> p (j k)")
+        C1 = 6.28125
+        C2 = 2.0 * math.pi - C1
+        turns_i = keep.tile([P, NA], I32)
+        nc.vector.tensor_scalar(
+            out=turns_i[:], in0=angf, scalar1=1.0 / (2.0 * math.pi), scalar2=0.25, op0=ALU.mult, op1=ALU.add
+        )
+        turns = keep.tile([P, NA], F32)
+        nc.vector.tensor_copy(out=turns[:], in_=turns_i[:])
+        red1 = keep.tile([P, NA], F32)
+        nc.vector.scalar_tensor_tensor(out=red1[:], in0=turns[:], scalar=-C1, in1=angf, op0=ALU.mult, op1=ALU.add)
+        red = keep.tile([P, NA], F32)
+        nc.vector.scalar_tensor_tensor(out=red[:], in0=turns[:], scalar=-C2, in1=red1[:], op0=ALU.mult, op1=ALU.add)
+        negabs = keep.tile([P, NA], F32)
+        nc.vector.scalar_tensor_tensor(out=negabs[:], in0=red[:], scalar=-1.0, in1=red[:], op0=ALU.mult, op1=ALU.min)
+        carg = keep.tile([P, NA], F32)
+        nc.vector.tensor_scalar(
+            out=carg[:], in0=negabs[:], scalar1=0.5, scalar2=0.5 * math.pi, op0=ALU.mult, op1=ALU.add
+        )
+        sh = keep.tile([P, NA], F32)
+        nc.scalar.activation(out=sh[:], in_=red[:], func=ACT.Sin, scale=0.5)
+        chh = keep.tile([P, NA], F32)
+        nc.scalar.activation(out=chh[:], in_=carg[:], func=ACT.Sin)
+        sin_t = keep.tile([P, JT, NK, 2], F32)
+        cos_t = keep.tile([P, JT, NK, 2], F32)
+        sin_f = sin_t[:].rearrange("p j k e -> p (j k) e")
+        nc.vector.scalar_tensor_tensor(out=sin_f[:, :, 1], in0=sh[:], scalar=2.0, in1=chh[:], op0=ALU.mult, op1=ALU.mult)
+        nc.vector.scalar_tensor_tensor(out=sin_f[:, :, 0], in0=sh[:], scalar=-2.0, in1=chh[:], op0=ALU.mult, op1=ALU.mult)
+        sq = keep.tile([P, NA], F32)
+        nc.vector.scalar_tensor_tensor(out=sq[:], in0=sh[:], scalar=-2.0, in1=sh[:], op0=ALU.mult, op1=ALU.mult)
+        nc.vector.tensor_scalar(
+            out=cos_t[:].rearrange("p j k e -> p (j k) e"),
+            in0=sq[:].unsqueeze(2).to_broadcast([P, NA, 2]),
+            scalar1=1.0,
+            scalar2=None,
+            op0=ALU.add,
+        )
+
+        xc = keep.tile([P, B * JT, PASSES, P], U32, align_bytes=64)
+        xs = keep.tile([P, B * JT, PASSES, P], U8, align_bytes=64)
+        wc = keep.tile([P, NCH, PASSES, CH], U32, align_bytes=64)
+        ws = keep.tile([P, NCH, PASSES, CH], U8, align_bytes=64)
+        kvc = keep.tile([P, PASSES, 2 * HD], U32, align_bytes=64)
+        kvs = keep.tile([P, PASSES, 2 * HD], U8, align_bytes=64)
+
+        def interleave(eng, out, in_):
+            if eng == "V":
+                nc.vector.tensor_copy(out=out, in_=in_)
+            elif eng == "S":
+                nc.scalar.copy(out=out, in_=in_)
+            else:
+                nc.gpsimd.tensor_scalar(out=out, in0=in_, scalar1=1.0, scalar2=0.0, op0=ALU.mult, op1=ALU.add)
+
+        def prep_wq(c):
+            for g in range(PASSES):
+                planes = plane_pool.tile([P, PACK, CH], BF16)
+                for t in range(PACK):
+                    src = wbytes[(c, g)][:, t, :].bitcast(FP8)
+                    if WIDEN.get((c, g), "S") == "S":
+                        nc.scalar.activation(out=planes[:, t, :], in_=src, func=ACT.Copy, scale=wsc[:, g, t : t + 1])
+                    else:
+                        nc.vector.tensor_scalar(
+                            out=planes[:, t, :], in0=src, scalar1=wsc[:, g, t : t + 1], scalar2=None, op0=ALU.mult
+                        )
+                grouped = group_pool.tile([P, CH, PACK], BF16, align_bytes=64)
+                interleave(INTER.get((c, g), "S"), grouped[:], planes[:].rearrange("p t n -> p n t"))
+                nc.vector.quantize_mx(
+                    out=wc[:, c, g, :].bitcast(FP8X4),
+                    scales=ws[:, c, g, :],
+                    in_=grouped[:].rearrange("p n t -> p (n t)"),
+                )
+
+        def prep_kv():
+            kvg = keep.tile([P, PASSES, 2, HD, PACK], BF16, align_bytes=64)
+            for g in range(PASSES):
+                interleave("G", kvg[:, g], kvr[:, :, g].rearrange("p w t n -> p w n t"))
+            nc.vector.quantize_mx(
+                out=kvc[:].rearrange("p g n -> p (g n)").bitcast(FP8X4),
+                scales=kvs[:].rearrange("p g n -> p (g n)"),
+                in_=kvg[:].rearrange("p g w n t -> p (g w n t)"),
+            )
+
+        def prep_x(b):
+            for j in range(JT):
+                xt = psx.tile([P, PASSES, 2, P], F32)
+                words = xr[(b, j // 2)][:, j % 2, :].bitcast(F32)
+                for g in range(PASSES):
+                    for u in range(2):
+                        nc.tensor.transpose(
+                            out=xt[:, g, u, :], in_=words[:, 256 * g + u : 256 * (g + 1) : 2], identity=ident[:]
+                        )
+                xg = xg_pool.tile([P, PASSES, P, 2], F32, align_bytes=64)
+                if XCOPY[b] == "V":
+                    nc.vector.tensor_copy(out=xg[:], in_=xt[:].rearrange("p g u r -> p g r u"))
+                else:
+                    nc.scalar.copy(out=xg[:], in_=xt[:].rearrange("p g u r -> p g r u"))
+                i = b * JT + j
+                nc.vector.quantize_mx(
+                    out=xc[:, i].rearrange("p g r -> p (g r)").bitcast(FP8X4),
+                    scales=xs[:, i].rearrange("p g r -> p (g r)"),
+                    in_=xg[:].rearrange("p g r u -> p (g r u)").bitcast(BF16),
+                )
+
+        def rope(acc4, m1, m2, cos4, sin4):
+            nc.vector.tensor_tensor(out=m1, in0=acc4, in1=cos4, op=ALU.mult)
+            nc.vector.tensor_tensor(out=m2, in0=acc4[:, :, :, ::-1], in1=sin4, op=ALU.mult)
+
+        def kv_chunk(b):
+            km1 = kv_pool.tile([P, JT, HD], F32)
+            km2 = kv_pool.tile([P, JT, HD], F32)
+            vo = kv_pool.tile([P, JT, HD], F32)
+            for jh in range(2):
+                acc = psa.tile([P, 2, 2 * HD], F32, name="acc")
+                for jj in range(2):
+                    i = b * JT + 2 * jh + jj
+                    for g in range(PASSES):
+                        nc.tensor.matmul_mx(
+                            out=acc[:, jj, :],
+                            lhsT=xc[:, i, g, :].bitcast(FP8X4),
+                            lhsT_scale=xs[:, i, g, :],
+                            rhs=kvc[:, g, :].bitcast(FP8X4),
+                            rhs_scale=kvs[:, g, :],
+                            start=(g == 0),
+                            stop=(g == PASSES - 1),
+                        )
+                js = slice(2 * jh, 2 * jh + 2)
+                rope(
+                    acc[:, :, 0:HD].rearrange("p a (k e) -> p a k e", e=2),
+                    km1[:, js, :].rearrange("p a (k e) -> p a k e", e=2),
+                    km2[:, js, :].rearrange("p a (k e) -> p a k e", e=2),
+                    cos_t[:, js],
+                    sin_t[:, js],
+                )
+                nc.scalar.copy(out=vo[:, js, :], in_=acc[:, :, HD : 2 * HD])
+            nc.gpsimd.tensor_tensor(out=km1[:], in0=km1[:], in1=km2[:], op=ALU.add)
+            nc.sync.dma_start(
+                out=out_1[b].rearrange("(p j) d -> p (j d)", j=JT), in_=km1[:].rearrange("p j d -> p (j d)")
+            )
+            nc.sync.dma_start(
+                out=out_2[b].rearrange("(p j) d -> p (j d)", j=JT), in_=vo[:].rearrange("p j d -> p (j d)")
+            )
+
+        def q_chunk(c, b):
+            m1 = prod_pool.tile([P, HPC, JT, HD], F32)
+            m2 = prod_pool.tile([P, HPC, JT, HD], F32)
+            for j in range(JT):
+                i = b * JT + j
+                acc = psa.tile([P, CH], F32, name="acc")
+                for g in range(PASSES):
+                    nc.tensor.matmul_mx(
+                        out=acc[:],
+                        lhsT=xc[:, i, g, :].bitcast(FP8X4),
+                        lhsT_scale=xs[:, i, g, :],
+                        rhs=wc[:, c, g, :].bitcast(FP8X4),
+                        rhs_scale=ws[:, c, g, :],
+                        start=(g == 0),
+                        stop=(g == PASSES - 1),
+                    )
+                rope(
+                    acc[:].rearrange("p (h k e) -> p h k e", h=HPC, e=2),
+                    m1[:, :, j, :].rearrange("p h (k e) -> p h k e", e=2),
+                    m2[:, :, j, :].rearrange("p h (k e) -> p h k e", e=2),
+                    cos_t[:, j : j + 1].to_broadcast([P, HPC, NK, 2]),
+                    sin_t[:, j : j + 1].to_broadcast([P, HPC, NK, 2]),
+                )
+                if (c, b, j) in VADD:
+                    nc.vector.tensor_tensor(out=m1[:, :, j, :], in0=m1[:, :, j, :], in1=m2[:, :, j, :], op=ALU.add)
+                else:
+                    nc.gpsimd.tensor_tensor(out=m1[:, :, j, :], in0=m1[:, :, j, :], in1=m2[:, :, j, :], op=ALU.add)
+                if (c, b) in FINE_STORE:
+                    nc.sync.dma_start(
+                        out=out_0[b, c * HPC : (c + 1) * HPC].rearrange("h (p j) d -> p h j d", j=JT)[:, :, j, :],
+                        in_=m1[:, :, j, :],
+                    )
+            if (c, b) not in FINE_STORE:
+                nc.sync.dma_start(
+                    out=out_0[b, c * HPC : (c + 1) * HPC].rearrange("h (p j) d -> p h (j d)", j=JT),
+                    in_=m1[:].rearrange("p h j d -> p h (j d)"),
+                )
+
+        prep_wq(0)
+        prep_x(0)
+        prep_kv()
+        kv_chunk(0)
+        prep_x(1)
+        kv_chunk(1)
+        for c in range(NCH):
+            if c + 1 < NCH:
+                prep_wq(c + 1)
+            for b in range(B):
+                q_chunk(c, b)

@@ -26,12 +26,7 @@ CH = 512
 NCH = HD * NH // CH
 HPC = CH // HD
 NK = HD // 2
-
-WIDEN = {(0, 1): "V"}
-INTER = {(0, 0): "G", (0, 1): "V"}
-XCOPY = {0: "S", 1: "S"}
-VADD = {(3, 1, 2), (3, 1, 3)}
-FINE_STORE = {(3, 1)}
+AHEAD = 2
 
 
 def tile_groupropeattention_pa_kernel(tc, x, Wq_bytes, Wq_scale, Wk, Wv, out_0, out_1, out_2):
@@ -40,12 +35,11 @@ def tile_groupropeattention_pa_kernel(tc, x, Wq_bytes, Wq_scale, Wk, Wv, out_0, 
         keep = ctx.enter_context(tc.tile_pool(name="keep", bufs=1))
         bytes_pool = ctx.enter_context(tc.tile_pool(name="bytes_pool", bufs=NCH * PASSES))
         plane_pool = ctx.enter_context(tc.tile_pool(name="plane_pool", bufs=3))
-        group_pool = ctx.enter_context(tc.tile_pool(name="group_pool", bufs=3))
-        xg_pool = ctx.enter_context(tc.tile_pool(name="xg_pool", bufs=3))
-        prod_pool = ctx.enter_context(tc.tile_pool(name="prod_pool", bufs=3))
+        group_pool = ctx.enter_context(tc.tile_pool(name="group_pool", bufs=2))
+        prod_pool = ctx.enter_context(tc.tile_pool(name="prod_pool", bufs=5))
         kv_pool = ctx.enter_context(tc.tile_pool(name="kv_pool", bufs=2))
-        psx = ctx.enter_context(tc.psum_pool(name="psx", bufs=2))
-        psa = ctx.enter_context(tc.psum_pool(name="psa", bufs=6))
+        psum = ctx.enter_context(tc.psum_pool(name="psum", bufs=8))
+        ctx.enter_context(tc.manual_schedule())
 
         pos = keep.tile([P, JT], F32)
         nc.gpsimd.iota(pos[:], pattern=[[1, JT]], base=0, channel_multiplier=JT, allow_small_or_imprecise_dtypes=True)
@@ -78,6 +72,9 @@ def tile_groupropeattention_pa_kernel(tc, x, Wq_bytes, Wq_scale, Wk, Wv, out_0, 
 
         load_wq(0)
         load_x(0)
+        load_x(1)
+        for c in range(1, NCH):
+            load_wq(c)
         kvr = keep.tile([P, 2, PASSES, PACK, HD], BF16)
         nc.sync.dma_start(
             out=kvr[:, 0].rearrange("p g t n -> p g (t n)"), in_=Wk.rearrange("(g p t) n -> p g (t n)", p=P, t=PACK)
@@ -85,56 +82,69 @@ def tile_groupropeattention_pa_kernel(tc, x, Wq_bytes, Wq_scale, Wk, Wv, out_0, 
         nc.sync.dma_start(
             out=kvr[:, 1].rearrange("p g t n -> p g (t n)"), in_=Wv.rearrange("(g p t) n -> p g (t n)", p=P, t=PACK)
         )
-        load_x(1)
-        for c in range(1, NCH):
-            load_wq(c)
 
         NA = JT * NK
-        ang = keep.tile([P, JT, NK], F32)
-        nc.vector.tensor_copy(out=ang[:, :, 0:1], in_=pos[:].unsqueeze(2))
-        w = 1
-        while w < NK:
-            nc.vector.tensor_scalar(
-                out=ang[:, :, w : 2 * w], in0=ang[:, :, 0:w], scalar1=THETA ** (-2.0 * w / HD), scalar2=None, op0=ALU.mult
-            )
-            w *= 2
-        angf = ang[:].rearrange("p j k -> p (j k)")
-        C1 = 6.28125
-        C2 = 2.0 * math.pi - C1
-        turns_i = keep.tile([P, NA], I32)
-        nc.vector.tensor_scalar(
-            out=turns_i[:], in0=angf, scalar1=1.0 / (2.0 * math.pi), scalar2=0.25, op0=ALU.mult, op1=ALU.add
-        )
-        turns = keep.tile([P, NA], F32)
-        nc.vector.tensor_copy(out=turns[:], in_=turns_i[:])
-        red1 = keep.tile([P, NA], F32)
-        nc.vector.scalar_tensor_tensor(out=red1[:], in0=turns[:], scalar=-C1, in1=angf, op0=ALU.mult, op1=ALU.add)
         red = keep.tile([P, NA], F32)
-        nc.vector.scalar_tensor_tensor(out=red[:], in0=turns[:], scalar=-C2, in1=red1[:], op0=ALU.mult, op1=ALU.add)
-        negabs = keep.tile([P, NA], F32)
-        nc.vector.scalar_tensor_tensor(out=negabs[:], in0=red[:], scalar=-1.0, in1=red[:], op0=ALU.mult, op1=ALU.min)
         carg = keep.tile([P, NA], F32)
-        nc.vector.tensor_scalar(
-            out=carg[:], in0=negabs[:], scalar1=0.5, scalar2=0.5 * math.pi, op0=ALU.mult, op1=ALU.add
-        )
         sh = keep.tile([P, NA], F32)
-        nc.scalar.activation(out=sh[:], in_=red[:], func=ACT.Sin, scale=0.5)
         chh = keep.tile([P, NA], F32)
-        nc.scalar.activation(out=chh[:], in_=carg[:], func=ACT.Sin)
         sin_t = keep.tile([P, JT, NK, 2], F32)
         cos_t = keep.tile([P, JT, NK, 2], F32)
-        sin_f = sin_t[:].rearrange("p j k e -> p (j k) e")
-        nc.vector.scalar_tensor_tensor(out=sin_f[:, :, 1], in0=sh[:], scalar=2.0, in1=chh[:], op0=ALU.mult, op1=ALU.mult)
-        nc.vector.scalar_tensor_tensor(out=sin_f[:, :, 0], in0=sh[:], scalar=-2.0, in1=chh[:], op0=ALU.mult, op1=ALU.mult)
-        sq = keep.tile([P, NA], F32)
-        nc.vector.scalar_tensor_tensor(out=sq[:], in0=sh[:], scalar=-2.0, in1=sh[:], op0=ALU.mult, op1=ALU.mult)
-        nc.vector.tensor_scalar(
-            out=cos_t[:].rearrange("p j k e -> p (j k) e"),
-            in0=sq[:].unsqueeze(2).to_broadcast([P, NA, 2]),
-            scalar1=1.0,
-            scalar2=None,
-            op0=ALU.add,
-        )
+
+        def tables_angles():
+            ang = keep.tile([P, JT, NK], F32)
+            nc.vector.tensor_copy(out=ang[:, :, 0:1], in_=pos[:].unsqueeze(2))
+            w = 1
+            while w < NK:
+                nc.vector.tensor_scalar(
+                    out=ang[:, :, w : 2 * w],
+                    in0=ang[:, :, 0:w],
+                    scalar1=THETA ** (-2.0 * w / HD),
+                    scalar2=None,
+                    op0=ALU.mult,
+                )
+                w *= 2
+            angf = ang[:].rearrange("p j k -> p (j k)")
+            c1 = 6.28125
+            c2 = 2.0 * math.pi - c1
+            turns_i = keep.tile([P, NA], I32)
+            nc.vector.tensor_scalar(
+                out=turns_i[:], in0=angf, scalar1=1.0 / (2.0 * math.pi), scalar2=0.25, op0=ALU.mult, op1=ALU.add
+            )
+            turns = keep.tile([P, NA], F32)
+            nc.vector.tensor_copy(out=turns[:], in_=turns_i[:])
+            red1 = keep.tile([P, NA], F32)
+            nc.vector.scalar_tensor_tensor(out=red1[:], in0=turns[:], scalar=-c1, in1=angf, op0=ALU.mult, op1=ALU.add)
+            nc.vector.scalar_tensor_tensor(out=red[:], in0=turns[:], scalar=-c2, in1=red1[:], op0=ALU.mult, op1=ALU.add)
+            negabs = keep.tile([P, NA], F32)
+            nc.vector.scalar_tensor_tensor(
+                out=negabs[:], in0=red[:], scalar=-1.0, in1=red[:], op0=ALU.mult, op1=ALU.min
+            )
+            nc.vector.tensor_scalar(
+                out=carg[:], in0=negabs[:], scalar1=0.5, scalar2=0.5 * math.pi, op0=ALU.mult, op1=ALU.add
+            )
+
+        def tables_sines():
+            nc.scalar.activation(out=sh[:], in_=red[:], func=ACT.Sin, scale=0.5)
+            nc.scalar.activation(out=chh[:], in_=carg[:], func=ACT.Sin)
+
+        def tables_finish():
+            sin_f = sin_t[:].rearrange("p j k e -> p (j k) e")
+            nc.vector.scalar_tensor_tensor(
+                out=sin_f[:, :, 1], in0=sh[:], scalar=2.0, in1=chh[:], op0=ALU.mult, op1=ALU.mult
+            )
+            nc.vector.scalar_tensor_tensor(
+                out=sin_f[:, :, 0], in0=sh[:], scalar=-2.0, in1=chh[:], op0=ALU.mult, op1=ALU.mult
+            )
+            sq = keep.tile([P, NA], F32)
+            nc.vector.scalar_tensor_tensor(out=sq[:], in0=sh[:], scalar=-2.0, in1=sh[:], op0=ALU.mult, op1=ALU.mult)
+            nc.vector.tensor_scalar(
+                out=cos_t[:].rearrange("p j k e -> p (j k) e"),
+                in0=sq[:].unsqueeze(2).to_broadcast([P, NA, 2]),
+                scalar1=1.0,
+                scalar2=None,
+                op0=ALU.add,
+            )
 
         xc = keep.tile([P, B * JT, PASSES, P], U32, align_bytes=64)
         xs = keep.tile([P, B * JT, PASSES, P], U8, align_bytes=64)
@@ -142,150 +152,199 @@ def tile_groupropeattention_pa_kernel(tc, x, Wq_bytes, Wq_scale, Wk, Wv, out_0, 
         ws = keep.tile([P, NCH, PASSES, CH], U8, align_bytes=64)
         kvc = keep.tile([P, PASSES, 2 * HD], U32, align_bytes=64)
         kvs = keep.tile([P, PASSES, 2 * HD], U8, align_bytes=64)
+        xg = keep.tile([P, B * JT, PASSES, P, 2], F32, align_bytes=64)
+        kvg = keep.tile([P, PASSES, 2, HD, PACK], BF16, align_bytes=64)
+        planes_of = {}
+        grouped_of = {}
+        xt_of = {}
 
-        def interleave(eng, out, in_):
+        def widen(c, g, eng):
+            planes = plane_pool.tile([P, PACK, CH], BF16)
+            planes_of[(c, g)] = planes
+            for t in range(PACK):
+                src = wbytes[(c, g)][:, t, :].bitcast(FP8)
+                if eng == "S":
+                    nc.scalar.activation(out=planes[:, t, :], in_=src, func=ACT.Copy, scale=wsc[:, g, t : t + 1])
+                else:
+                    nc.vector.tensor_scalar(
+                        out=planes[:, t, :], in0=src, scalar1=wsc[:, g, t : t + 1], scalar2=None, op0=ALU.mult
+                    )
+
+        def new_group(c):
+            grouped = group_pool.tile([P, PASSES, CH, PACK], BF16, align_bytes=64)
+            grouped_of[c] = grouped
+
+        def inter(c, g, eng):
+            src = planes_of[(c, g)][:].rearrange("p t n -> p n t")
             if eng == "V":
-                nc.vector.tensor_copy(out=out, in_=in_)
-            elif eng == "S":
-                nc.scalar.copy(out=out, in_=in_)
+                nc.vector.tensor_copy(out=grouped_of[c][:, g], in_=src)
             else:
-                nc.gpsimd.tensor_scalar(out=out, in0=in_, scalar1=1.0, scalar2=0.0, op0=ALU.mult, op1=ALU.add)
+                nc.scalar.copy(out=grouped_of[c][:, g], in_=src)
 
-        def prep_wq(c):
-            for g in range(PASSES):
-                planes = plane_pool.tile([P, PACK, CH], BF16)
-                for t in range(PACK):
-                    src = wbytes[(c, g)][:, t, :].bitcast(FP8)
-                    if WIDEN.get((c, g), "S") == "S":
-                        nc.scalar.activation(out=planes[:, t, :], in_=src, func=ACT.Copy, scale=wsc[:, g, t : t + 1])
-                    else:
-                        nc.vector.tensor_scalar(
-                            out=planes[:, t, :], in0=src, scalar1=wsc[:, g, t : t + 1], scalar2=None, op0=ALU.mult
-                        )
-                grouped = group_pool.tile([P, CH, PACK], BF16, align_bytes=64)
-                interleave(INTER.get((c, g), "S"), grouped[:], planes[:].rearrange("p t n -> p n t"))
-                nc.vector.quantize_mx(
-                    out=wc[:, c, g, :].bitcast(FP8X4),
-                    scales=ws[:, c, g, :],
-                    in_=grouped[:].rearrange("p n t -> p (n t)"),
-                )
+        def quant_w(c):
+            nc.vector.quantize_mx(
+                out=wc[:, c].rearrange("p g n -> p (g n)").bitcast(FP8X4),
+                scales=ws[:, c].rearrange("p g n -> p (g n)"),
+                in_=grouped_of[c][:].rearrange("p g n t -> p (g n t)"),
+            )
 
-        def prep_kv():
-            kvg = keep.tile([P, PASSES, 2, HD, PACK], BF16, align_bytes=64)
+        def prep_on_scalar(c):
+            new_group(c)
             for g in range(PASSES):
-                interleave("G", kvg[:, g], kvr[:, :, g].rearrange("p w t n -> p w n t"))
+                widen(c, g, "S")
+                inter(c, g, "S")
+
+        def kv_inter():
+            for g in range(PASSES):
+                nc.scalar.copy(out=kvg[:, g], in_=kvr[:, :, g].rearrange("p w t n -> p w n t"))
+
+        def kv_quant():
             nc.vector.quantize_mx(
                 out=kvc[:].rearrange("p g n -> p (g n)").bitcast(FP8X4),
                 scales=kvs[:].rearrange("p g n -> p (g n)"),
                 in_=kvg[:].rearrange("p g w n t -> p (g w n t)"),
             )
 
-        def prep_x(b):
-            for j in range(JT):
-                xt = psx.tile([P, PASSES, 2, P], F32)
-                words = xr[(b, j // 2)][:, j % 2, :].bitcast(F32)
-                for g in range(PASSES):
-                    for u in range(2):
-                        nc.tensor.transpose(
-                            out=xt[:, g, u, :], in_=words[:, 256 * g + u : 256 * (g + 1) : 2], identity=ident[:]
-                        )
-                xg = xg_pool.tile([P, PASSES, P, 2], F32, align_bytes=64)
-                if XCOPY[b] == "V":
-                    nc.vector.tensor_copy(out=xg[:], in_=xt[:].rearrange("p g u r -> p g r u"))
-                else:
-                    nc.scalar.copy(out=xg[:], in_=xt[:].rearrange("p g u r -> p g r u"))
-                i = b * JT + j
-                nc.vector.quantize_mx(
-                    out=xc[:, i].rearrange("p g r -> p (g r)").bitcast(FP8X4),
-                    scales=xs[:, i].rearrange("p g r -> p (g r)"),
-                    in_=xg[:].rearrange("p g r u -> p (g r u)").bitcast(BF16),
+        def x_transposes(i):
+            xt = psum.tile([P, PASSES, 2, P], F32, name="bank")
+            xt_of[i] = xt
+            words = xr[(i // JT, (i % JT) // 2)][:, i % 2, :].bitcast(F32)
+            for g in range(PASSES):
+                for u in range(2):
+                    nc.tensor.transpose(
+                        out=xt[:, g, u, :], in_=words[:, 256 * g + u : 256 * (g + 1) : 2], identity=ident[:]
+                    )
+
+        def x_copy(i):
+            nc.scalar.copy(out=xg[:, i], in_=xt_of[i][:].rearrange("p g u r -> p g r u"))
+
+        def x_quant(i0, n):
+            nc.vector.quantize_mx(
+                out=xc[:, i0 : i0 + n].rearrange("p i g r -> p (i g r)").bitcast(FP8X4),
+                scales=xs[:, i0 : i0 + n].rearrange("p i g r -> p (i g r)"),
+                in_=xg[:, i0 : i0 + n].rearrange("p i g r u -> p (i g r u)").bitcast(BF16),
+            )
+
+        banks = [("Q", c, b, j) for c in range(NCH) for b in range(B) for j in range(JT)]
+        banks += [("K", b, jh) for b in range(B) for jh in range(2)]
+        acc_of = {}
+        prod_of = {}
+
+        def passes(out, i, rhs, rhs_scale):
+            for g in range(PASSES):
+                nc.tensor.matmul_mx(
+                    out=out,
+                    lhsT=xc[:, i, g, :].bitcast(FP8X4),
+                    lhsT_scale=xs[:, i, g, :],
+                    rhs=rhs[:, g, :].bitcast(FP8X4),
+                    rhs_scale=rhs_scale[:, g, :],
+                    start=(g == 0),
+                    stop=(g == PASSES - 1),
                 )
 
-        def rope(acc4, m1, m2, cos4, sin4):
+        def matmuls(bank):
+            if bank[0] == "Q":
+                c, b, j = bank[1:]
+                acc = psum.tile([P, CH], F32, name="bank")
+                passes(acc[:], b * JT + j, wc[:, c], ws[:, c])
+            else:
+                b, jh = bank[1:]
+                acc = psum.tile([P, 2, 2 * HD], F32, name="bank")
+                for jj in range(2):
+                    passes(acc[:, jj, :], b * JT + 2 * jh + jj, kvc, kvs)
+            acc_of[bank] = acc
+
+        def products(acc4, m1, m2, cos4, sin4):
             nc.vector.tensor_tensor(out=m1, in0=acc4, in1=cos4, op=ALU.mult)
             nc.vector.tensor_tensor(out=m2, in0=acc4[:, :, :, ::-1], in1=sin4, op=ALU.mult)
 
-        def kv_chunk(b):
-            km1 = kv_pool.tile([P, JT, HD], F32)
-            km2 = kv_pool.tile([P, JT, HD], F32)
-            vo = kv_pool.tile([P, JT, HD], F32)
-            for jh in range(2):
-                acc = psa.tile([P, 2, 2 * HD], F32, name="acc")
-                for jj in range(2):
-                    i = b * JT + 2 * jh + jj
-                    for g in range(PASSES):
-                        nc.tensor.matmul_mx(
-                            out=acc[:, jj, :],
-                            lhsT=xc[:, i, g, :].bitcast(FP8X4),
-                            lhsT_scale=xs[:, i, g, :],
-                            rhs=kvc[:, g, :].bitcast(FP8X4),
-                            rhs_scale=kvs[:, g, :],
-                            start=(g == 0),
-                            stop=(g == PASSES - 1),
-                        )
+        def rope(bank):
+            acc = acc_of[bank]
+            if bank[0] == "Q":
+                c, b, j = bank[1:]
+                if j % 2 == 0:
+                    m1 = prod_pool.tile([P, HPC, 2, HD], F32)
+                    m2 = prod_pool.tile([P, HPC, 2, HD], F32)
+                    prod_of[(c, b)] = (m1, m2)
+                m1, m2 = prod_of[(c, b)]
+                products(
+                    acc[:].rearrange("p (h k e) -> p h k e", h=HPC, e=2),
+                    m1[:, :, j % 2, :].rearrange("p h (k e) -> p h k e", e=2),
+                    m2[:, :, j % 2, :].rearrange("p h (k e) -> p h k e", e=2),
+                    cos_t[:, j : j + 1].to_broadcast([P, HPC, NK, 2]),
+                    sin_t[:, j : j + 1].to_broadcast([P, HPC, NK, 2]),
+                )
+                if j % 2 == 1:
+                    nc.gpsimd.tensor_tensor(out=m1[:], in0=m1[:], in1=m2[:], op=ALU.add)
+                    nc.sync.dma_start(
+                        out=out_0[b, c * HPC : (c + 1) * HPC].rearrange("h (p j) d -> p h (j d)", j=JT)[
+                            :, :, (j - 1) * HD : (j + 1) * HD
+                        ],
+                        in_=m1[:].rearrange("p h a d -> p h (a d)"),
+                    )
+            else:
+                b, jh = bank[1:]
+                if jh == 0:
+                    km1 = kv_pool.tile([P, JT, HD], F32)
+                    km2 = kv_pool.tile([P, JT, HD], F32)
+                    vo = kv_pool.tile([P, JT, HD], F32)
+                    prod_of[("K", b)] = (km1, km2, vo)
+                km1, km2, vo = prod_of[("K", b)]
                 js = slice(2 * jh, 2 * jh + 2)
-                rope(
+                nc.scalar.copy(out=vo[:, js, :], in_=acc[:, :, HD : 2 * HD])
+                products(
                     acc[:, :, 0:HD].rearrange("p a (k e) -> p a k e", e=2),
                     km1[:, js, :].rearrange("p a (k e) -> p a k e", e=2),
                     km2[:, js, :].rearrange("p a (k e) -> p a k e", e=2),
                     cos_t[:, js],
                     sin_t[:, js],
                 )
-                nc.scalar.copy(out=vo[:, js, :], in_=acc[:, :, HD : 2 * HD])
-            nc.gpsimd.tensor_tensor(out=km1[:], in0=km1[:], in1=km2[:], op=ALU.add)
-            nc.sync.dma_start(
-                out=out_1[b].rearrange("(p j) d -> p (j d)", j=JT), in_=km1[:].rearrange("p j d -> p (j d)")
-            )
-            nc.sync.dma_start(
-                out=out_2[b].rearrange("(p j) d -> p (j d)", j=JT), in_=vo[:].rearrange("p j d -> p (j d)")
-            )
-
-        def q_chunk(c, b):
-            m1 = prod_pool.tile([P, HPC, JT, HD], F32)
-            m2 = prod_pool.tile([P, HPC, JT, HD], F32)
-            for j in range(JT):
-                i = b * JT + j
-                acc = psa.tile([P, CH], F32, name="acc")
-                for g in range(PASSES):
-                    nc.tensor.matmul_mx(
-                        out=acc[:],
-                        lhsT=xc[:, i, g, :].bitcast(FP8X4),
-                        lhsT_scale=xs[:, i, g, :],
-                        rhs=wc[:, c, g, :].bitcast(FP8X4),
-                        rhs_scale=ws[:, c, g, :],
-                        start=(g == 0),
-                        stop=(g == PASSES - 1),
-                    )
-                rope(
-                    acc[:].rearrange("p (h k e) -> p h k e", h=HPC, e=2),
-                    m1[:, :, j, :].rearrange("p h (k e) -> p h k e", e=2),
-                    m2[:, :, j, :].rearrange("p h (k e) -> p h k e", e=2),
-                    cos_t[:, j : j + 1].to_broadcast([P, HPC, NK, 2]),
-                    sin_t[:, j : j + 1].to_broadcast([P, HPC, NK, 2]),
-                )
-                if (c, b, j) in VADD:
-                    nc.vector.tensor_tensor(out=m1[:, :, j, :], in0=m1[:, :, j, :], in1=m2[:, :, j, :], op=ALU.add)
-                else:
-                    nc.gpsimd.tensor_tensor(out=m1[:, :, j, :], in0=m1[:, :, j, :], in1=m2[:, :, j, :], op=ALU.add)
-                if (c, b) in FINE_STORE:
+                if b == B - 1:
+                    nc.vector.tensor_tensor(out=km1[:, js, :], in0=km1[:, js, :], in1=km2[:, js, :], op=ALU.add)
+                elif jh == 1:
+                    nc.gpsimd.tensor_tensor(out=km1[:], in0=km1[:], in1=km2[:], op=ALU.add)
+                if jh == 1:
                     nc.sync.dma_start(
-                        out=out_0[b, c * HPC : (c + 1) * HPC].rearrange("h (p j) d -> p h j d", j=JT)[:, :, j, :],
-                        in_=m1[:, :, j, :],
+                        out=out_2[b].rearrange("(p j) d -> p (j d)", j=JT), in_=vo[:].rearrange("p j d -> p (j d)")
                     )
-            if (c, b) not in FINE_STORE:
-                nc.sync.dma_start(
-                    out=out_0[b, c * HPC : (c + 1) * HPC].rearrange("h (p j) d -> p h (j d)", j=JT),
-                    in_=m1[:].rearrange("p h j d -> p h (j d)"),
-                )
+                    nc.sync.dma_start(
+                        out=out_1[b].rearrange("(p j) d -> p (j d)", j=JT), in_=km1[:].rearrange("p j d -> p (j d)")
+                    )
 
-        prep_wq(0)
-        prep_x(0)
-        prep_kv()
-        kv_chunk(0)
-        prep_x(1)
-        kv_chunk(1)
-        for c in range(NCH):
-            if c + 1 < NCH:
-                prep_wq(c + 1)
-            for b in range(B):
-                q_chunk(c, b)
+        tables_angles()
+        new_group(0)
+        widen(0, 0, "S")
+        widen(0, 1, "V")
+        tables_sines()
+        inter(0, 1, "V")
+        tables_finish()
+        for i in range(B * JT):
+            x_transposes(i)
+        x_copy(0)
+        x_quant(0, 1)
+        inter(0, 0, "V")
+        x_copy(1)
+        x_quant(1, 1)
+        quant_w(0)
+        x_copy(2)
+        x_copy(3)
+        x_quant(2, 2)
+        for i in range(JT, B * JT):
+            x_copy(i)
+        prep_on_scalar(1)
+        for n in range(AHEAD):
+            matmuls(banks[n])
+        for n in range(len(banks)):
+            if n == 2:
+                x_quant(JT, JT)
+            if n % 8 == 6 and n // 8 + 1 < NCH:
+                quant_w(n // 8 + 1)
+                if n // 8 + 2 < NCH:
+                    prep_on_scalar(n // 8 + 2)
+                else:
+                    kv_inter()
+            if n == NCH * B * JT - AHEAD:
+                kv_quant()
+            if n + AHEAD < len(banks):
+                matmuls(banks[n + AHEAD])
+            rope(banks[n])

@@ -175,11 +175,12 @@ def tile_groupropeattention_pa_kernel(tc, x, Wq_bytes, Wq_scale, Wk, Wv, out_0, 
             grouped_of[c] = grouped
 
         def inter(c, g, eng):
-            src = planes_of[(c, g)][:].rearrange("p t n -> p n t")
+            src = planes_of[(c, g)][:].rearrange("p t (q i) -> p q t i", i=4)
+            dst = grouped_of[c][:, g].rearrange("p (q i) t -> p q t i", i=4)
             if eng == "V":
-                nc.vector.tensor_copy(out=grouped_of[c][:, g], in_=src)
+                nc.vector.tensor_copy(out=dst, in_=src)
             else:
-                nc.scalar.copy(out=grouped_of[c][:, g], in_=src)
+                nc.scalar.copy(out=dst, in_=src)
 
         def quant_w(c):
             nc.vector.quantize_mx(
@@ -299,14 +300,18 @@ def tile_groupropeattention_pa_kernel(tc, x, Wq_bytes, Wq_scale, Wk, Wv, out_0, 
                     cos_t[:, js],
                     sin_t[:, js],
                 )
-                if b == B - 1:
-                    nc.vector.tensor_tensor(out=km1[:, js, :], in0=km1[:, js, :], in1=km2[:, js, :], op=ALU.add)
-                elif jh == 1:
-                    nc.gpsimd.tensor_tensor(out=km1[:], in0=km1[:], in1=km2[:], op=ALU.add)
                 if jh == 1:
                     nc.sync.dma_start(
                         out=out_2[b].rearrange("(p j) d -> p (j d)", j=JT), in_=vo[:].rearrange("p j d -> p (j d)")
                     )
+                if b == B - 1:
+                    nc.vector.tensor_tensor(out=km1[:, js, :], in0=km1[:, js, :], in1=km2[:, js, :], op=ALU.add)
+                    nc.sync.dma_start(
+                        out=out_1[b].rearrange("(p j) d -> p j d", j=JT)[:, js, :].rearrange("p j d -> p (j d)"),
+                        in_=km1[:, js, :].rearrange("p j d -> p (j d)"),
+                    )
+                elif jh == 1:
+                    nc.gpsimd.tensor_tensor(out=km1[:], in0=km1[:], in1=km2[:], op=ALU.add)
                     nc.sync.dma_start(
                         out=out_1[b].rearrange("(p j) d -> p (j d)", j=JT), in_=km1[:].rearrange("p j d -> p (j d)")
                     )

@@ -41,8 +41,10 @@ def tile_groupropeattention_pa_kernel(tc, x, Wq_bytes, Wq_scale, Wk, Wv, out_0, 
         psum = ctx.enter_context(tc.psum_pool(name="psum", bufs=8))
         ctx.enter_context(tc.manual_schedule())
 
-        pos = keep.tile([P, JT], F32)
-        nc.gpsimd.iota(pos[:], pattern=[[1, JT]], base=0, channel_multiplier=JT, allow_small_or_imprecise_dtypes=True)
+        ang = keep.tile([P, JT, NK], F32)
+        nc.gpsimd.iota(
+            ang[:, :, 0:1], pattern=[[1, JT]], base=0, channel_multiplier=JT, allow_small_or_imprecise_dtypes=True
+        )
         zero1 = keep.tile([P, 1], F32)
         nc.gpsimd.memset(zero1[:], 0.0)
         warm = keep.tile([P, 1], F32)
@@ -51,7 +53,7 @@ def tile_groupropeattention_pa_kernel(tc, x, Wq_bytes, Wq_scale, Wk, Wv, out_0, 
         make_identity(nc, ident[:])
 
         wsc = keep.tile([P, PASSES, PACK], F32)
-        nc.sync.dma_start(out=wsc[:], in_=Wq_scale.rearrange("(g p t) o -> p g (t o)", p=P, t=PACK))
+        nc.scalar.dma_start(out=wsc[:], in_=Wq_scale.rearrange("(g p t) o -> p g (t o)", p=P, t=PACK))
         wq_view = Wq_bytes.rearrange("(g p t) n -> g p t n", p=P, t=PACK)
         wbytes = {}
 
@@ -91,9 +93,15 @@ def tile_groupropeattention_pa_kernel(tc, x, Wq_bytes, Wq_scale, Wk, Wv, out_0, 
         sin_t = keep.tile([P, JT, NK, 2], F32)
         cos_t = keep.tile([P, JT, NK, 2], F32)
 
+        angf = ang[:].rearrange("p j k -> p (j k)")
+        c1 = 6.28125
+        c2 = 2.0 * math.pi - c1
+        turns_i = keep.tile([P, NA], I32)
+        turns = keep.tile([P, NA], F32)
+        red1 = keep.tile([P, NA], F32)
+        negabs = keep.tile([P, NA], F32)
+
         def tables_angles():
-            ang = keep.tile([P, JT, NK], F32)
-            nc.vector.tensor_copy(out=ang[:, :, 0:1], in_=pos[:].unsqueeze(2))
             w = 1
             while w < NK:
                 nc.vector.tensor_scalar(
@@ -104,25 +112,30 @@ def tile_groupropeattention_pa_kernel(tc, x, Wq_bytes, Wq_scale, Wk, Wv, out_0, 
                     op0=ALU.mult,
                 )
                 w *= 2
-            angf = ang[:].rearrange("p j k -> p (j k)")
-            c1 = 6.28125
-            c2 = 2.0 * math.pi - c1
-            turns_i = keep.tile([P, NA], I32)
-            nc.vector.tensor_scalar(
-                out=turns_i[:], in0=angf, scalar1=1.0 / (2.0 * math.pi), scalar2=0.25, op0=ALU.mult, op1=ALU.add
-            )
-            turns = keep.tile([P, NA], F32)
-            nc.vector.tensor_copy(out=turns[:], in_=turns_i[:])
-            red1 = keep.tile([P, NA], F32)
-            nc.vector.scalar_tensor_tensor(out=red1[:], in0=turns[:], scalar=-c1, in1=angf, op0=ALU.mult, op1=ALU.add)
-            nc.vector.scalar_tensor_tensor(out=red[:], in0=turns[:], scalar=-c2, in1=red1[:], op0=ALU.mult, op1=ALU.add)
-            negabs = keep.tile([P, NA], F32)
-            nc.vector.scalar_tensor_tensor(
-                out=negabs[:], in0=red[:], scalar=-1.0, in1=red[:], op0=ALU.mult, op1=ALU.min
-            )
-            nc.vector.tensor_scalar(
-                out=carg[:], in0=negabs[:], scalar1=0.5, scalar2=0.5 * math.pi, op0=ALU.mult, op1=ALU.add
-            )
+
+        def reduce_step(s):
+            if s == 0:
+                nc.vector.tensor_scalar(
+                    out=turns_i[:], in0=angf, scalar1=1.0 / (2.0 * math.pi), scalar2=0.25, op0=ALU.mult, op1=ALU.add
+                )
+            elif s == 1:
+                nc.vector.tensor_copy(out=turns[:], in_=turns_i[:])
+            elif s == 2:
+                nc.vector.scalar_tensor_tensor(
+                    out=red1[:], in0=turns[:], scalar=-c1, in1=angf, op0=ALU.mult, op1=ALU.add
+                )
+            elif s == 3:
+                nc.vector.scalar_tensor_tensor(
+                    out=red[:], in0=turns[:], scalar=-c2, in1=red1[:], op0=ALU.mult, op1=ALU.add
+                )
+            elif s == 4:
+                nc.vector.scalar_tensor_tensor(
+                    out=negabs[:], in0=red[:], scalar=-1.0, in1=red[:], op0=ALU.mult, op1=ALU.min
+                )
+            else:
+                nc.vector.tensor_scalar(
+                    out=carg[:], in0=negabs[:], scalar1=0.5, scalar2=0.5 * math.pi, op0=ALU.mult, op1=ALU.add
+                )
 
         def tables_sines():
             nc.scalar.activation(out=sh[:], in_=red[:], func=ACT.Sin, scale=0.5)
@@ -169,6 +182,7 @@ def tile_groupropeattention_pa_kernel(tc, x, Wq_bytes, Wq_scale, Wk, Wv, out_0, 
                     nc.vector.tensor_scalar(
                         out=planes[:, t, :], in0=src, scalar1=wsc[:, g, t : t + 1], scalar2=None, op0=ALU.mult
                     )
+                    reduce_step(t)
 
         def new_group(c):
             grouped = group_pool.tile([P, PASSES, CH, PACK], BF16, align_bytes=64)
@@ -320,16 +334,18 @@ def tile_groupropeattention_pa_kernel(tc, x, Wq_bytes, Wq_scale, Wk, Wv, out_0, 
         new_group(0)
         widen(0, 0, "S")
         widen(0, 1, "V")
-        tables_sines()
-        inter(0, 1, "V")
-        tables_finish()
         for i in range(B * JT):
             x_transposes(i)
         x_copy(0)
-        x_quant(0, 1)
-        inter(0, 0, "V")
         x_copy(1)
+        inter(0, 1, "V")
+        reduce_step(4)
+        x_quant(0, 1)
+        reduce_step(5)
+        tables_sines()
+        inter(0, 0, "V")
         x_quant(1, 1)
+        tables_finish()
         quant_w(0)
         x_copy(2)
         x_copy(3)

@@ -27,6 +27,9 @@ NCH = HD * NH // CH
 HPC = CH // HD
 NK = HD // 2
 AHEAD = 2
+WARM_FIRST = 10
+WARM_BETWEEN = 2
+X_FIRST = 6
 
 
 def tile_groupropeattention_pa_kernel(tc, x, Wq_bytes, Wq_scale, Wk, Wv, out_0, out_1, out_2):
@@ -38,7 +41,8 @@ def tile_groupropeattention_pa_kernel(tc, x, Wq_bytes, Wq_scale, Wk, Wv, out_0, 
         group_pool = ctx.enter_context(tc.tile_pool(name="group_pool", bufs=2))
         prod_pool = ctx.enter_context(tc.tile_pool(name="prod_pool", bufs=5))
         kv_pool = ctx.enter_context(tc.tile_pool(name="kv_pool", bufs=2))
-        psum = ctx.enter_context(tc.psum_pool(name="psum", bufs=8))
+        psum = ctx.enter_context(tc.psum_pool(name="psum", bufs=7))
+        psum_idle = ctx.enter_context(tc.psum_pool(name="psum_idle", bufs=1))
         ctx.enter_context(tc.manual_schedule())
 
         ang = keep.tile([P, JT, NK], F32)
@@ -49,18 +53,32 @@ def tile_groupropeattention_pa_kernel(tc, x, Wq_bytes, Wq_scale, Wk, Wv, out_0, 
         nc.gpsimd.memset(zero1[:], 0.0)
         warm = keep.tile([P, 1], F32)
         nc.scalar.activation(out=warm[:], in_=zero1[:], func=ACT.Sin)
+        zeros = keep.tile([P, CH], BF16)
+        nc.gpsimd.memset(zeros[:], 0.0)
         ident = keep.tile([P, P], F32)
         make_identity(nc, ident[:])
+        idle_bank = psum_idle.tile([P, CH], F32)
+
+        def keep_clock(n):
+            for r in range(n):
+                nc.tensor.matmul(out=idle_bank[:], lhsT=zeros[:, 0:P], rhs=zeros[:], start=True, stop=True)
+
+        keep_clock(WARM_FIRST)
 
         wsc = keep.tile([P, PASSES, PACK], F32)
-        nc.scalar.dma_start(out=wsc[:], in_=Wq_scale.rearrange("(g p t) o -> p g (t o)", p=P, t=PACK))
+        nc.sync.dma_start(out=wsc[:], in_=Wq_scale.rearrange("(g p t) o -> p g (t o)", p=P, t=PACK))
         wq_view = Wq_bytes.rearrange("(g p t) n -> g p t n", p=P, t=PACK)
         wbytes = {}
 
         def load_wq(c):
             for g in range(PASSES):
                 wq_codes_in = bytes_pool.tile([P, PACK, CH], U8)
-                nc.sync.dma_start(out=wq_codes_in[:], in_=wq_view[g][:, :, c * CH : (c + 1) * CH])
+                cuts = 2 if (c, g) == (0, 0) else 1
+                step = PACK // cuts
+                for t0 in range(0, PACK, step):
+                    nc.sync.dma_start(
+                        out=wq_codes_in[:, t0 : t0 + step, :], in_=wq_view[g][:, t0 : t0 + step, c * CH : (c + 1) * CH]
+                    )
                 wbytes[(c, g)] = wq_codes_in
 
         xr = {}
@@ -143,14 +161,14 @@ def tile_groupropeattention_pa_kernel(tc, x, Wq_bytes, Wq_scale, Wk, Wv, out_0, 
 
         def tables_finish():
             sin_f = sin_t[:].rearrange("p j k e -> p (j k) e")
+            sq = keep.tile([P, NA], F32)
+            nc.vector.scalar_tensor_tensor(out=sq[:], in0=sh[:], scalar=-2.0, in1=sh[:], op0=ALU.mult, op1=ALU.mult)
             nc.vector.scalar_tensor_tensor(
                 out=sin_f[:, :, 1], in0=sh[:], scalar=2.0, in1=chh[:], op0=ALU.mult, op1=ALU.mult
             )
             nc.vector.scalar_tensor_tensor(
                 out=sin_f[:, :, 0], in0=sh[:], scalar=-2.0, in1=chh[:], op0=ALU.mult, op1=ALU.mult
             )
-            sq = keep.tile([P, NA], F32)
-            nc.vector.scalar_tensor_tensor(out=sq[:], in0=sh[:], scalar=-2.0, in1=sh[:], op0=ALU.mult, op1=ALU.mult)
             nc.vector.tensor_scalar(
                 out=cos_t[:].rearrange("p j k e -> p (j k) e"),
                 in0=sq[:].unsqueeze(2).to_broadcast([P, NA, 2]),
@@ -332,29 +350,38 @@ def tile_groupropeattention_pa_kernel(tc, x, Wq_bytes, Wq_scale, Wk, Wv, out_0, 
 
         tables_angles()
         new_group(0)
-        widen(0, 0, "S")
-        widen(0, 1, "V")
-        for i in range(B * JT):
+        widen(0, 0, "V")
+        widen(0, 1, "S")
+        for i in range(X_FIRST):
             x_transposes(i)
+            if i % 2 == 1:
+                keep_clock(WARM_BETWEEN)
         x_copy(0)
         x_copy(1)
-        inter(0, 1, "V")
+        inter(0, 0, "V")
         reduce_step(4)
         x_quant(0, 1)
         reduce_step(5)
         tables_sines()
-        inter(0, 0, "V")
+        inter(0, 1, "V")
         x_quant(1, 1)
-        tables_finish()
         quant_w(0)
+        tables_finish()
         x_copy(2)
         x_copy(3)
         x_quant(2, 2)
-        for i in range(JT, B * JT):
+        for i in range(JT, X_FIRST):
             x_copy(i)
-        prep_on_scalar(1)
+        new_group(1)
+        widen(1, 0, "S")
         for n in range(AHEAD):
             matmuls(banks[n])
+        for i in range(X_FIRST, B * JT):
+            x_transposes(i)
+            x_copy(i)
+        inter(1, 0, "S")
+        widen(1, 1, "S")
+        inter(1, 1, "S")
         for n in range(len(banks)):
             if n == 2:
                 x_quant(JT, JT)

@@ -30,6 +30,7 @@ AHEAD = 2
 WARM_FIRST = 10
 WARM_BETWEEN = 2
 X_FIRST = 6
+PIECES = ((0, 0, CH),) + tuple((c, col0, CH // 2) for c in range(1, NCH) for col0 in (0, CH // 2))
 
 
 def tile_groupropeattention_pa_kernel(tc, x, Wq_bytes, Wq_scale, Wk, Wv, out_0, out_1, out_2):
@@ -38,7 +39,7 @@ def tile_groupropeattention_pa_kernel(tc, x, Wq_bytes, Wq_scale, Wk, Wv, out_0, 
         keep = ctx.enter_context(tc.tile_pool(name="keep", bufs=1))
         bytes_pool = ctx.enter_context(tc.tile_pool(name="bytes_pool", bufs=NCH * PASSES))
         plane_pool = ctx.enter_context(tc.tile_pool(name="plane_pool", bufs=3))
-        group_pool = ctx.enter_context(tc.tile_pool(name="group_pool", bufs=2))
+        group_pool = ctx.enter_context(tc.tile_pool(name="group_pool", bufs=4))
         prod_pool = ctx.enter_context(tc.tile_pool(name="prod_pool", bufs=5))
         kv_pool = ctx.enter_context(tc.tile_pool(name="kv_pool", bufs=2))
         psum = ctx.enter_context(tc.psum_pool(name="psum", bufs=7))
@@ -189,11 +190,12 @@ def tile_groupropeattention_pa_kernel(tc, x, Wq_bytes, Wq_scale, Wk, Wv, out_0, 
         grouped_of = {}
         xt_of = {}
 
-        def widen(c, g, eng):
-            planes = plane_pool.tile([P, PACK, CH], BF16)
-            planes_of[(c, g)] = planes
+        def widen(s, g, eng):
+            c, col0, width = PIECES[s]
+            planes = plane_pool.tile([P, PACK, width], BF16)
+            planes_of[(s, g)] = planes
             for t in range(PACK):
-                src = wbytes[(c, g)][:, t, :].bitcast(FP8)
+                src = wbytes[(c, g)][:, t, col0 : col0 + width].bitcast(FP8)
                 if eng == "S":
                     nc.scalar.activation(out=planes[:, t, :], in_=src, func=ACT.Copy, scale=wsc[:, g, t : t + 1])
                 else:
@@ -202,9 +204,17 @@ def tile_groupropeattention_pa_kernel(tc, x, Wq_bytes, Wq_scale, Wk, Wv, out_0, 
                     )
                     reduce_step(t)
 
-        def new_group(c):
-            grouped = group_pool.tile([P, PASSES, CH, PACK], BF16, align_bytes=64)
-            grouped_of[c] = grouped
+        def new_group(s):
+            grouped = group_pool.tile([P, PASSES, PIECES[s][2], PACK], BF16, align_bytes=64)
+            grouped_of[s] = grouped
+
+        def codes(s):
+            c, col0, width = PIECES[s]
+            span = slice(PASSES * col0, PASSES * (col0 + width))
+            return (
+                wc[:, c].rearrange("p g n -> p (g n)")[:, span],
+                ws[:, c].rearrange("p g n -> p (g n)")[:, span],
+            )
 
         def inter(c, g, eng):
             src = planes_of[(c, g)][:].rearrange("p t (q i) -> p q t i", i=4)
@@ -214,11 +224,12 @@ def tile_groupropeattention_pa_kernel(tc, x, Wq_bytes, Wq_scale, Wk, Wv, out_0, 
             else:
                 nc.scalar.copy(out=dst, in_=src)
 
-        def quant_w(c):
+        def quant_w(s):
+            words, scale_bytes = codes(s)
             nc.vector.quantize_mx(
-                out=wc[:, c].rearrange("p g n -> p (g n)").bitcast(FP8X4),
-                scales=ws[:, c].rearrange("p g n -> p (g n)"),
-                in_=grouped_of[c][:].rearrange("p g n t -> p (g n t)"),
+                out=words.bitcast(FP8X4),
+                scales=scale_bytes,
+                in_=grouped_of[s][:].rearrange("p g n t -> p (g n t)"),
             )
 
         def prep_on_scalar(c):
@@ -258,7 +269,11 @@ def tile_groupropeattention_pa_kernel(tc, x, Wq_bytes, Wq_scale, Wk, Wv, out_0, 
                 in_=xg[:, i0 : i0 + n].rearrange("p i g r u -> p (i g r u)").bitcast(BF16),
             )
 
-        banks = [("Q", c, b, j) for c in range(NCH) for b in range(B) for j in range(JT)]
+        banks = []
+        first_bank = []
+        for s in range(len(PIECES)):
+            first_bank += [len(banks)]
+            banks += [("Q", s, b, jb) for b in range(B) for jb in range(JT * PIECES[s][2] // CH)]
         banks += [("K", b, jh) for b in range(B) for jh in range(2)]
         acc_of = {}
         prod_of = {}
@@ -277,9 +292,18 @@ def tile_groupropeattention_pa_kernel(tc, x, Wq_bytes, Wq_scale, Wk, Wv, out_0, 
 
         def matmuls(bank):
             if bank[0] == "Q":
-                c, b, j = bank[1:]
-                acc = psum.tile([P, CH], F32, name="bank")
-                passes(acc[:], b * JT + j, wc[:, c], ws[:, c])
+                s, b, jb = bank[1:]
+                width = PIECES[s][2]
+                tpb = CH // width
+                words, scale_bytes = codes(s)
+                acc = psum.tile([P, tpb, width], F32, name="bank")
+                for a in range(tpb):
+                    passes(
+                        acc[:, a, :],
+                        b * JT + jb * tpb + a,
+                        words.rearrange("p (g n) -> p g n", g=PASSES),
+                        scale_bytes.rearrange("p (g n) -> p g n", g=PASSES),
+                    )
             else:
                 b, jh = bank[1:]
                 acc = psum.tile([P, 2, 2 * HD], F32, name="bank")
@@ -291,27 +315,47 @@ def tile_groupropeattention_pa_kernel(tc, x, Wq_bytes, Wq_scale, Wk, Wv, out_0, 
             nc.vector.tensor_tensor(out=m1, in0=acc4, in1=cos4, op=ALU.mult)
             nc.vector.tensor_tensor(out=m2, in0=acc4[:, :, :, ::-1], in1=sin4, op=ALU.mult)
 
+        def products5(acc5, m1, m2, cos5, sin5):
+            nc.vector.tensor_tensor(out=m1, in0=acc5, in1=cos5, op=ALU.mult)
+            nc.vector.tensor_tensor(out=m2, in0=acc5[:, :, :, :, ::-1], in1=sin5, op=ALU.mult)
+
         def rope(bank):
             acc = acc_of[bank]
             if bank[0] == "Q":
-                c, b, j = bank[1:]
-                if j % 2 == 0:
-                    m1 = prod_pool.tile([P, HPC, 2, HD], F32)
-                    m2 = prod_pool.tile([P, HPC, 2, HD], F32)
-                    prod_of[(c, b)] = (m1, m2)
-                m1, m2 = prod_of[(c, b)]
-                products(
-                    acc[:].rearrange("p (h k e) -> p h k e", h=HPC, e=2),
-                    m1[:, :, j % 2, :].rearrange("p h (k e) -> p h k e", e=2),
-                    m2[:, :, j % 2, :].rearrange("p h (k e) -> p h k e", e=2),
-                    cos_t[:, j : j + 1].to_broadcast([P, HPC, NK, 2]),
-                    sin_t[:, j : j + 1].to_broadcast([P, HPC, NK, 2]),
-                )
-                if j % 2 == 1:
+                s, b, jb = bank[1:]
+                c, col0, width = PIECES[s]
+                nh = width // HD
+                tpb = CH // width
+                half = jb % 2
+                if half == 0:
+                    m1 = prod_pool.tile([P, nh, 2 * tpb, HD], F32)
+                    m2 = prod_pool.tile([P, nh, 2 * tpb, HD], F32)
+                    prod_of[(s, b)] = (m1, m2)
+                m1, m2 = prod_of[(s, b)]
+                j0 = jb * tpb
+                if tpb == 1:
+                    products(
+                        acc[:, 0, :].rearrange("p (h k e) -> p h k e", h=nh, e=2),
+                        m1[:, :, half, :].rearrange("p h (k e) -> p h k e", e=2),
+                        m2[:, :, half, :].rearrange("p h (k e) -> p h k e", e=2),
+                        cos_t[:, j0 : j0 + 1].to_broadcast([P, nh, NK, 2]),
+                        sin_t[:, j0 : j0 + 1].to_broadcast([P, nh, NK, 2]),
+                    )
+                else:
+                    mine = slice(half * tpb, (half + 1) * tpb)
+                    products5(
+                        acc[:].rearrange("p a (h k e) -> p a h k e", h=nh, e=2),
+                        m1[:, :, mine, :].rearrange("p h a (k e) -> p a h k e", e=2),
+                        m2[:, :, mine, :].rearrange("p h a (k e) -> p a h k e", e=2),
+                        cos_t[:, j0 : j0 + tpb].unsqueeze(2).to_broadcast([P, tpb, nh, NK, 2]),
+                        sin_t[:, j0 : j0 + tpb].unsqueeze(2).to_broadcast([P, tpb, nh, NK, 2]),
+                    )
+                if half == 1:
+                    head0 = (c * CH + col0) // HD
                     nc.gpsimd.tensor_tensor(out=m1[:], in0=m1[:], in1=m2[:], op=ALU.add)
                     nc.sync.dma_start(
-                        out=out_0[b, c * HPC : (c + 1) * HPC].rearrange("h (p j) d -> p h (j d)", j=JT)[
-                            :, :, (j - 1) * HD : (j + 1) * HD
+                        out=out_0[b, head0 : head0 + nh].rearrange("h (p j) d -> p h (j d)", j=JT)[
+                            :, :, (j0 - tpb) * HD : (j0 + tpb) * HD
                         ],
                         in_=m1[:].rearrange("p h a d -> p h (a d)"),
                     )
@@ -385,10 +429,11 @@ def tile_groupropeattention_pa_kernel(tc, x, Wq_bytes, Wq_scale, Wk, Wv, out_0, 
         for n in range(len(banks)):
             if n == 2:
                 x_quant(JT, JT)
-            if n % 8 == 6 and n // 8 + 1 < NCH:
-                quant_w(n // 8 + 1)
-                if n // 8 + 2 < NCH:
-                    prep_on_scalar(n // 8 + 2)
+            if n + AHEAD in first_bank[1:]:
+                s = first_bank.index(n + AHEAD)
+                quant_w(s)
+                if s + 1 < len(PIECES):
+                    prep_on_scalar(s + 1)
                 else:
                     kv_inter()
             if n == NCH * B * JT - AHEAD:

@@ -138,27 +138,21 @@ def tile_groupropeattention_pa_kernel(tc, x, Wq_bytes, Wq_scale, Wk, Wv, out_0, 
                     out=turns_i[:], in0=angf, scalar1=1.0 / (2.0 * math.pi), scalar2=0.25, op0=ALU.mult, op1=ALU.add
                 )
             elif s == 1:
-                nc.vector.tensor_copy(out=turns[:], in_=turns_i[:])
+                nc.vector.scalar_tensor_tensor(
+                    out=red1[:], in0=turns_i[:], scalar=-c1, in1=angf, op0=ALU.mult, op1=ALU.add
+                )
             elif s == 2:
                 nc.vector.scalar_tensor_tensor(
-                    out=red1[:], in0=turns[:], scalar=-c1, in1=angf, op0=ALU.mult, op1=ALU.add
-                )
-            elif s == 3:
-                nc.vector.scalar_tensor_tensor(
-                    out=red[:], in0=turns[:], scalar=-c2, in1=red1[:], op0=ALU.mult, op1=ALU.add
-                )
-            elif s == 4:
-                nc.vector.scalar_tensor_tensor(
-                    out=negabs[:], in0=red[:], scalar=-1.0, in1=red[:], op0=ALU.mult, op1=ALU.min
+                    out=red[:], in0=turns_i[:], scalar=-c2, in1=red1[:], op0=ALU.mult, op1=ALU.add
                 )
             else:
-                nc.vector.tensor_scalar(
-                    out=carg[:], in0=negabs[:], scalar1=0.5, scalar2=0.5 * math.pi, op0=ALU.mult, op1=ALU.add
+                nc.vector.scalar_tensor_tensor(
+                    out=negabs[:], in0=red[:], scalar=-1.0, in1=red[:], op0=ALU.mult, op1=ALU.min
                 )
 
         def tables_sines():
             nc.scalar.activation(out=sh[:], in_=red[:], func=ACT.Sin, scale=0.5)
-            nc.scalar.activation(out=chh[:], in_=carg[:], func=ACT.Sin)
+            nc.scalar.activation(out=chh[:], in_=negabs[:], func=ACT.Sin, scale=0.5, bias=0.5 * math.pi)
 
         def tables_finish():
             sin_f = sin_t[:].rearrange("p j k e -> p (j k) e")
@@ -403,9 +397,7 @@ def tile_groupropeattention_pa_kernel(tc, x, Wq_bytes, Wq_scale, Wk, Wv, out_0, 
         x_copy(0)
         x_copy(1)
         inter(0, 0, "V")
-        reduce_step(4)
         x_quant(0, 1)
-        reduce_step(5)
         tables_sines()
         inter(0, 1, "V")
         x_quant(1, 1)

@@ -153,23 +153,21 @@ def tile_groupropeattention_pa_kernel(tc, x, Wq_bytes, Wq_scale, Wk, Wv, out_0, 
         def tables_sines():
             nc.scalar.activation(out=sh[:], in_=red[:], func=ACT.Sin, scale=0.5)
             nc.scalar.activation(out=chh[:], in_=negabs[:], func=ACT.Sin, scale=0.5, bias=0.5 * math.pi)
+            nc.scalar.activation(
+                out=cos_t[:].rearrange("p j k e -> p (j k) e"),
+                in_=negabs[:].unsqueeze(2).to_broadcast([P, NA, 2]),
+                func=ACT.Sin,
+                bias=0.5 * math.pi,
+            )
 
         def tables_finish():
             sin_f = sin_t[:].rearrange("p j k e -> p (j k) e")
             sq = keep.tile([P, NA], F32)
-            nc.vector.scalar_tensor_tensor(out=sq[:], in0=sh[:], scalar=-2.0, in1=sh[:], op0=ALU.mult, op1=ALU.mult)
             nc.vector.scalar_tensor_tensor(
                 out=sin_f[:, :, 1], in0=sh[:], scalar=2.0, in1=chh[:], op0=ALU.mult, op1=ALU.mult
             )
             nc.vector.scalar_tensor_tensor(
                 out=sin_f[:, :, 0], in0=sh[:], scalar=-2.0, in1=chh[:], op0=ALU.mult, op1=ALU.mult
-            )
-            nc.vector.tensor_scalar(
-                out=cos_t[:].rearrange("p j k e -> p (j k) e"),
-                in0=sq[:].unsqueeze(2).to_broadcast([P, NA, 2]),
-                scalar1=1.0,
-                scalar2=None,
-                op0=ALU.add,
             )
 
         xc = keep.tile([P, B * JT, PASSES, P], U32, align_bytes=64)

@@ -106,63 +106,44 @@ def tile_groupropeattention_pa_kernel(tc, x, Wq_bytes, Wq_scale, Wk, Wv, out_0, 
 
         NA = JT * NK
         red = keep.tile([P, NA], F32)
-        carg = keep.tile([P, NA], F32)
         sh = keep.tile([P, NA], F32)
         chh = keep.tile([P, NA], F32)
         sin_t = keep.tile([P, JT, NK, 2], F32)
         cos_t = keep.tile([P, JT, NK, 2], F32)
-
-        angf = ang[:].rearrange("p j k -> p (j k)")
-        c1 = 6.28125
-        c2 = 2.0 * math.pi - c1
         turns_i = keep.tile([P, NA], I32)
-        turns = keep.tile([P, NA], F32)
-        red1 = keep.tile([P, NA], F32)
-        negabs = keep.tile([P, NA], F32)
+        angf = ang[:].rearrange("p j k -> p (j k)")
 
         def tables_angles():
             w = 1
             while w < NK:
-                nc.vector.tensor_scalar(
-                    out=ang[:, :, w : 2 * w],
-                    in0=ang[:, :, 0:w],
-                    scalar1=THETA ** (-2.0 * w / HD),
-                    scalar2=None,
-                    op0=ALU.mult,
-                )
-                w *= 2
-
-        def reduce_step(s):
-            if s == 0:
-                nc.vector.tensor_scalar(
-                    out=turns_i[:], in0=angf, scalar1=1.0 / (2.0 * math.pi), scalar2=0.25, op0=ALU.mult, op1=ALU.add
-                )
-            elif s == 1:
-                nc.vector.scalar_tensor_tensor(
-                    out=red1[:], in0=turns_i[:], scalar=-c1, in1=angf, op0=ALU.mult, op1=ALU.add
-                )
-            elif s == 2:
-                nc.vector.scalar_tensor_tensor(
-                    out=red[:], in0=turns_i[:], scalar=-c2, in1=red1[:], op0=ALU.mult, op1=ALU.add
-                )
-            else:
-                nc.vector.scalar_tensor_tensor(
-                    out=negabs[:], in0=red[:], scalar=-1.0, in1=red[:], op0=ALU.mult, op1=ALU.min
-                )
+                for m in range(1, 4):
+                    nc.vector.tensor_scalar(
+                        out=ang[:, :, m * w : (m + 1) * w],
+                        in0=ang[:, :, 0:w],
+                        scalar1=THETA ** (-2.0 * m * w / HD),
+                        scalar2=None,
+                        op0=ALU.mult,
+                    )
+                w *= 4
+            nc.vector.tensor_scalar(
+                out=turns_i[:], in0=angf, scalar1=1.0 / (2.0 * math.pi), scalar2=0.25, op0=ALU.mult, op1=ALU.add
+            )
+            nc.vector.scalar_tensor_tensor(
+                out=red[:], in0=turns_i[:], scalar=-2.0 * math.pi, in1=angf, op0=ALU.mult, op1=ALU.add
+            )
 
         def tables_sines():
             nc.scalar.activation(out=sh[:], in_=red[:], func=ACT.Sin, scale=0.5)
-            nc.scalar.activation(out=chh[:], in_=negabs[:], func=ACT.Sin, scale=0.5, bias=0.5 * math.pi)
+            nc.scalar.activation(out=chh[:], in_=red[:], func=ACT.Sin, scale=0.5, bias=0.5 * math.pi)
             nc.scalar.activation(
                 out=cos_t[:].rearrange("p j k e -> p (j k) e"),
-                in_=negabs[:].unsqueeze(2).to_broadcast([P, NA, 2]),
+                in_=red[:].unsqueeze(2).to_broadcast([P, NA, 2]),
                 func=ACT.Sin,
                 bias=0.5 * math.pi,
             )
 
         def tables_finish():
             sin_f = sin_t[:].rearrange("p j k e -> p (j k) e")
-            sq = keep.tile([P, NA], F32)
             nc.vector.scalar_tensor_tensor(
                 out=sin_f[:, :, 1], in0=sh[:], scalar=2.0, in1=chh[:], op0=ALU.mult, op1=ALU.mult
             )
@@ -182,19 +163,18 @@ def tile_groupropeattention_pa_kernel(tc, x, Wq_bytes, Wq_scale, Wk, Wv, out_0, 
         grouped_of = {}
         xt_of = {}
 
-        def widen(s, g, eng):
+        def widen(s, g, engines):
             c, col0, width = PIECES[s]
             planes = plane_pool.tile([P, PACK, width], BF16)
             planes_of[(s, g)] = planes
             for t in range(PACK):
                 src = wbytes[(c, g)][:, t, col0 : col0 + width].bitcast(FP8)
-                if eng == "S":
+                if engines[t] == "S":
                     nc.scalar.activation(out=planes[:, t, :], in_=src, func=ACT.Copy, scale=wsc[:, g, t : t + 1])
                 else:
                     nc.vector.tensor_scalar(
                         out=planes[:, t, :], in0=src, scalar1=wsc[:, g, t : t + 1], scalar2=None, op0=ALU.mult
                     )
-                    reduce_step(t)
 
         def new_group(s):
             grouped = group_pool.tile([P, PASSES, PIECES[s][2], PACK], BF16, align_bytes=64)
@@ -227,7 +207,7 @@ def tile_groupropeattention_pa_kernel(tc, x, Wq_bytes, Wq_scale, Wk, Wv, out_0, 
         def prep_on_scalar(c):
             new_group(c)
             for g in range(PASSES):
-                widen(c, g, "S")
+                widen(c, g, "SSSS")
                 inter(c, g, "S")
 
         def kv_inter():
@@ -386,8 +366,8 @@ def tile_groupropeattention_pa_kernel(tc, x, Wq_bytes, Wq_scale, Wk, Wv, out_0, 
 
         tables_angles()
         new_group(0)
-        widen(0, 0, "V")
-        widen(0, 1, "S")
+        widen(0, 0, "VVVV")
+        widen(0, 1, "SSVV")
         for i in range(X_FIRST):
             x_transposes(i)
             if i % 2 == 1:
@@ -395,11 +375,11 @@ def tile_groupropeattention_pa_kernel(tc, x, Wq_bytes, Wq_scale, Wk, Wv, out_0, 
         x_copy(0)
         x_copy(1)
         inter(0, 0, "V")
-        x_quant(0, 1)
-        tables_sines()
         inter(0, 1, "V")
-        x_quant(1, 1)
         quant_w(0)
+        x_quant(0, 1)
+        x_quant(1, 1)
+        tables_sines()
         tables_finish()
         x_copy(2)
         x_copy(3)
@@ -407,14 +387,14 @@ def tile_groupropeattention_pa_kernel(tc, x, Wq_bytes, Wq_scale, Wk, Wv, out_0, 
         for i in range(JT, X_FIRST):
             x_copy(i)
         new_group(1)
-        widen(1, 0, "S")
+        widen(1, 0, "SSSS")
         for n in range(AHEAD):
             matmuls(banks[n])
         for i in range(X_FIRST, B * JT):
             x_transposes(i)
             x_copy(i)
         inter(1, 0, "S")
-        widen(1, 1, "S")
+        widen(1, 1, "SSSS")
         inter(1, 1, "S")
         for n in range(len(banks)):
             if n == 2:

@@ -112,6 +112,10 @@ def tile_groupropeattention_pa_kernel(tc, x, Wq_bytes, Wq_scale, Wk, Wv, out_0, 
         cos_t = keep.tile([P, JT, NK, 2], F32)
         turns_i = keep.tile([P, NA], I32)
         angf = ang[:].rearrange("p j k -> p (j k)")
+        sin_a = keep.tile([P, NA], F32)
+        signs = keep.tile([P, 2], F32)
+        nc.vector.memset(signs[:, 0:1], -1.0)
+        nc.vector.memset(signs[:, 1:2], 1.0)
 
         def tables_angles():
             w = 1
@@ -143,12 +147,12 @@ def tile_groupropeattention_pa_kernel(tc, x, Wq_bytes, Wq_scale, Wk, Wv, out_0, 
             )
 
         def tables_finish():
-            sin_f = sin_t[:].rearrange("p j k e -> p (j k) e")
-            nc.vector.scalar_tensor_tensor(
-                out=sin_f[:, :, 1], in0=sh[:], scalar=2.0, in1=chh[:], op0=ALU.mult, op1=ALU.mult
-            )
-            nc.vector.scalar_tensor_tensor(
-                out=sin_f[:, :, 0], in0=sh[:], scalar=-2.0, in1=chh[:], op0=ALU.mult, op1=ALU.mult
+            nc.vector.scalar_tensor_tensor(out=sin_a[:], in0=sh[:], scalar=2.0, in1=chh[:], op0=ALU.mult, op1=ALU.mult)
+            nc.vector.tensor_tensor(
+                out=sin_t[:].rearrange("p j k e -> p (j k) e"),
+                in0=sin_a[:].unsqueeze(2).to_broadcast([P, NA, 2]),
+                in1=signs[:].unsqueeze(1).to_broadcast([P, NA, 2]),
+                op=ALU.mult,
             )
 
         xc = keep.tile([P, B * JT, PASSES, P], U32, align_bytes=64)
@@ -377,8 +381,7 @@ def tile_groupropeattention_pa_kernel(tc, x, Wq_bytes, Wq_scale, Wk, Wv, out_0, 
         inter(0, 0, "V")
         inter(0, 1, "V")
         quant_w(0)
-        x_quant(0, 1)
-        x_quant(1, 1)
+        x_quant(0, 2)
         tables_sines()
         tables_finish()
         x_copy(2)

import math
from contextlib import ExitStack

import concourse.mybir as mybir
from concourse.masks import make_identity

B, L, EMB, HD, NH = 2, 512, 1024, 128, 16
THETA = 10000.0
FLOPS = 2 * B * L * EMB * (HD * NH + 2 * HD)

F32 = mybir.dt.float32
BF16 = mybir.dt.bfloat16
I32 = mybir.dt.int32
U32 = mybir.dt.uint32
U8 = mybir.dt.uint8
FP8 = mybir.dt.float8_e4m3fn
FP8X4 = mybir.dt.float8_e4m3fn_x4
ALU = mybir.AluOpType
ACT = mybir.ActivationFunctionType

P = 128
PACK = 4
PASSES = EMB // (P * PACK)
JT = L // P
CH = 512
NCH = HD * NH // CH
HPC = CH // HD
NK = HD // 2
AHEAD = 2
WARM_FIRST = 10
WARM_BETWEEN = 2
X_FIRST = 6
PIECES = ((0, 0, CH),) + tuple((c, col0, CH // 2) for c in range(1, NCH) for col0 in (0, CH // 2))


def tile_groupropeattention_pa_kernel(tc, x, Wq_bytes, Wq_scale, Wk, Wv, out_0, out_1, out_2):
    nc = tc.nc
    with ExitStack() as ctx:
        keep = ctx.enter_context(tc.tile_pool(name="keep", bufs=1))
        bytes_pool = ctx.enter_context(tc.tile_pool(name="bytes_pool", bufs=NCH * PASSES))
        plane_pool = ctx.enter_context(tc.tile_pool(name="plane_pool", bufs=3))
        group_pool = ctx.enter_context(tc.tile_pool(name="group_pool", bufs=4))
        prod_pool = ctx.enter_context(tc.tile_pool(name="prod_pool", bufs=5))
        kv_pool = ctx.enter_context(tc.tile_pool(name="kv_pool", bufs=2))
        psum = ctx.enter_context(tc.psum_pool(name="psum", bufs=7))
        psum_idle = ctx.enter_context(tc.psum_pool(name="psum_idle", bufs=1))
        ctx.enter_context(tc.manual_schedule())

        ang = keep.tile([P, JT, NK], F32)
        nc.gpsimd.iota(
            ang[:, :, 0:1], pattern=[[1, JT]], base=0, channel_multiplier=JT, allow_small_or_imprecise_dtypes=True
        )
        zero1 = keep.tile([P, 1], F32)
        nc.gpsimd.memset(zero1[:], 0.0)
        warm = keep.tile([P, 1], F32)
        nc.scalar.activation(out=warm[:], in_=zero1[:], func=ACT.Sin)
        zeros = keep.tile([P, CH], BF16)
        nc.gpsimd.memset(zeros[:], 0.0)
        ident = keep.tile([P, P], F32)
        make_identity(nc, ident[:])
        idle_bank = psum_idle.tile([P, CH], F32)

        def keep_clock(n):
            for r in range(n):
                nc.tensor.matmul(out=idle_bank[:], lhsT=zeros[:, 0:P], rhs=zeros[:], start=True, stop=True)

        keep_clock(WARM_FIRST)

        wsc = keep.tile([P, PASSES, PACK], F32)
        nc.sync.dma_start(out=wsc[:], in_=Wq_scale.rearrange("(g p t) o -> p g (t o)", p=P, t=PACK))
        wq_view = Wq_bytes.rearrange("(g p t) n -> g p t n", p=P, t=PACK)
        wbytes = {}

        def load_wq(c):
            for g in range(PASSES):
                wq_codes_in = bytes_pool.tile([P, PACK, CH], U8)
                cuts = 2 if (c, g) == (0, 0) else 1
                step = PACK // cuts
                for t0 in range(0, PACK, step):
                    nc.sync.dma_start(
                        out=wq_codes_in[:, t0 : t0 + step, :], in_=wq_view[g][:, t0 : t0 + step, c * CH : (c + 1) * CH]
                    )
                wbytes[(c, g)] = wq_codes_in

        xr = {}

        def load_x(b):
            xv = x[b].rearrange("(p j) k -> p j k", j=JT)
            for jh in range(2):
                xraw = keep.tile([P, 2, EMB], BF16, name="xraw%d%d" % (b, jh))
                nc.sync.dma_start(out=xraw[:], in_=xv[:, 2 * jh : 2 * jh + 2, :])
                xr[(b, jh)] = xraw

        load_wq(0)
        load_x(0)
        load_x(1)
        for c in range(1, NCH):
            load_wq(c)
        kvr = keep.tile([P, 2, PASSES, PACK, HD], BF16)
        nc.sync.dma_start(
            out=kvr[:, 0].rearrange("p g t n -> p g (t n)"), in_=Wk.rearrange("(g p t) n -> p g (t n)", p=P, t=PACK)
        )
        nc.sync.dma_start(
            out=kvr[:, 1].rearrange("p g t n -> p g (t n)"), in_=Wv.rearrange("(g p t) n -> p g (t n)", p=P, t=PACK)
        )

        NA = JT * NK
        red = keep.tile([P, NA], F32)
        sh = keep.tile([P, NA], F32)
        chh = keep.tile([P, NA], F32)
        sin_t = keep.tile([P, JT, NK, 2], F32)
        cos_t = keep.tile([P, JT, NK, 2], F32)
        turns_i = keep.tile([P, NA], I32)
        angf = ang[:].rearrange("p j k -> p (j k)")
        sin_a = keep.tile([P, NA], F32)
        signs = keep.tile([P, 2], F32)
        nc.vector.memset(signs[:, 0:1], -1.0)
        nc.vector.memset(signs[:, 1:2], 1.0)

        def tables_angles():
            w = 1
            while w < NK:
                for m in range(1, 4):
                    nc.vector.tensor_scalar(
                        out=ang[:, :, m * w : (m + 1) * w],
                        in0=ang[:, :, 0:w],
                        scalar1=THETA ** (-2.0 * m * w / HD),
                        scalar2=None,
                        op0=ALU.mult,
                    )
                w *= 4
            nc.vector.tensor_scalar(
                out=turns_i[:], in0=angf, scalar1=1.0 / (2.0 * math.pi), scalar2=0.25, op0=ALU.mult, op1=ALU.add
            )
            nc.vector.scalar_tensor_tensor(
                out=red[:], in0=turns_i[:], scalar=-2.0 * math.pi, in1=angf, op0=ALU.mult, op1=ALU.add
            )

        def tables_sines():
            nc.scalar.activation(out=sh[:], in_=red[:], func=ACT.Sin, scale=0.5)
            nc.scalar.activation(out=chh[:], in_=red[:], func=ACT.Sin, scale=0.5, bias=0.5 * math.pi)
            nc.scalar.activation(
                out=cos_t[:].rearrange("p j k e -> p (j k) e"),
                in_=red[:].unsqueeze(2).to_broadcast([P, NA, 2]),
                func=ACT.Sin,
                bias=0.5 * math.pi,
            )

        def tables_finish():
            nc.vector.scalar_tensor_tensor(out=sin_a[:], in0=sh[:], scalar=2.0, in1=chh[:], op0=ALU.mult, op1=ALU.mult)
            nc.vector.tensor_tensor(
                out=sin_t[:].rearrange("p j k e -> p (j k) e"),
                in0=sin_a[:].unsqueeze(2).to_broadcast([P, NA, 2]),
                in1=signs[:].unsqueeze(1).to_broadcast([P, NA, 2]),
                op=ALU.mult,
            )

        xc = keep.tile([P, B * JT, PASSES, P], U32, align_bytes=64)
        xs = keep.tile([P, B * JT, PASSES, P], U8, align_bytes=64)
        wc = keep.tile([P, NCH, PASSES, CH], U32, align_bytes=64)
        ws = keep.tile([P, NCH, PASSES, CH], U8, align_bytes=64)
        kvc = keep.tile([P, PASSES, 2 * HD], U32, align_bytes=64)
        kvs = keep.tile([P, PASSES, 2 * HD], U8, align_bytes=64)
        xg = keep.tile([P, B * JT, PASSES, P, 2], F32, align_bytes=64)
        kvg = keep.tile([P, PASSES, 2, HD, PACK], BF16, align_bytes=64)
        planes_of = {}
        grouped_of = {}
        xt_of = {}

        def widen(s, g, engines):
            c, col0, width = PIECES[s]
            planes = plane_pool.tile([P, PACK, width], BF16)
            planes_of[(s, g)] = planes
            for t in range(PACK):
                src = wbytes[(c, g)][:, t, col0 : col0 + width].bitcast(FP8)
                if engines[t] == "S":
                    nc.scalar.activation(out=planes[:, t, :], in_=src, func=ACT.Copy, scale=wsc[:, g, t : t + 1])
                else:
                    nc.vector.tensor_scalar(
                        out=planes[:, t, :], in0=src, scalar1=wsc[:, g, t : t + 1], scalar2=None, op0=ALU.mult
                    )

        def new_group(s):
            grouped = group_pool.tile([P, PASSES, PIECES[s][2], PACK], BF16, align_bytes=64)
            grouped_of[s] = grouped

        def codes(s):
            c, col0, width = PIECES[s]
            span = slice(PASSES * col0, PASSES * (col0 + width))
            return (
                wc[:, c].rearrange("p g n -> p (g n)")[:, span],
                ws[:, c].rearrange("p g n -> p (g n)")[:, span],
            )

        def inter(c, g, eng):
            src = planes_of[(c, g)][:].rearrange("p t (q i) -> p q t i", i=4)
            dst = grouped_of[c][:, g].rearrange("p (q i) t -> p q t i", i=4)
            if eng == "V":
                nc.vector.tensor_copy(out=dst, in_=src)
            else:
                nc.scalar.copy(out=dst, in_=src)

        def quant_w(s):
            words, scale_bytes = codes(s)
            nc.vector.quantize_mx(
                out=words.bitcast(FP8X4),
                scales=scale_bytes,
                in_=grouped_of[s][:].rearrange("p g n t -> p (g n t)"),
            )

        def prep_on_scalar(c):
            new_group(c)
            for g in range(PASSES):
                widen(c, g, "SSSS")
                inter(c, g, "S")

        def kv_inter():
            for g in range(PASSES):
                nc.scalar.copy(out=kvg[:, g], in_=kvr[:, :, g].rearrange("p w t n -> p w n t"))

        def kv_quant():
            nc.vector.quantize_mx(
                out=kvc[:].rearrange("p g n -> p (g n)").bitcast(FP8X4),
                scales=kvs[:].rearrange("p g n -> p (g n)"),
                in_=kvg[:].rearrange("p g w n t -> p (g w n t)"),
            )

        def x_transposes(i):
            xt = psum.tile([P, PASSES, 2, P], F32, name="bank")
            xt_of[i] = xt
            words = xr[(i // JT, (i % JT) // 2)][:, i % 2, :].bitcast(F32)
            for g in range(PASSES):
                for u in range(2):
                    nc.tensor.transpose(
                        out=xt[:, g, u, :], in_=words[:, 256 * g + u : 256 * (g + 1) : 2], identity=ident[:]
                    )

        def x_copy(i):
            nc.scalar.copy(out=xg[:, i], in_=xt_of[i][:].rearrange("p g u r -> p g r u"))

        def x_quant(i0, n):
            nc.vector.quantize_mx(
                out=xc[:, i0 : i0 + n].rearrange("p i g r -> p (i g r)").bitcast(FP8X4),
                scales=xs[:, i0 : i0 + n].rearrange("p i g r -> p (i g r)"),
                in_=xg[:, i0 : i0 + n].rearrange("p i g r u -> p (i g r u)").bitcast(BF16),
            )

        banks = []
        first_bank = []
        for s in range(len(PIECES)):
            first_bank += [len(banks)]
            banks += [("Q", s, b, jb) for b in range(B) for jb in range(JT * PIECES[s][2] // CH)]
        banks += [("K", b, jh) for b in range(B) for jh in range(2)]
        acc_of = {}
        prod_of = {}

        def passes(out, i, rhs, rhs_scale):
            for g in range(PASSES):
                nc.tensor.matmul_mx(
                    out=out,
                    lhsT=xc[:, i, g, :].bitcast(FP8X4),
                    lhsT_scale=xs[:, i, g, :],
                    rhs=rhs[:, g, :].bitcast(FP8X4),
                    rhs_scale=rhs_scale[:, g, :],
                    start=(g == 0),
                    stop=(g == PASSES - 1),
                )

        def matmuls(bank):
            if bank[0] == "Q":
                s, b, jb = bank[1:]
                width = PIECES[s][2]
                tpb = CH // width
                words, scale_bytes = codes(s)
                acc = psum.tile([P, tpb, width], F32, name="bank")
                for a in range(tpb):
                    passes(
                        acc[:, a, :],
                        b * JT + jb * tpb + a,
                        words.rearrange("p (g n) -> p g n", g=PASSES),
                        scale_bytes.rearrange("p (g n) -> p g n", g=PASSES),
                    )
            else:
                b, jh = bank[1:]
                acc = psum.tile([P, 2, 2 * HD], F32, name="bank")
                for jj in range(2):
                    passes(acc[:, jj, :], b * JT + 2 * jh + jj, kvc, kvs)
            acc_of[bank] = acc

        def products(acc4, m1, m2, cos4, sin4):
            nc.vector.tensor_tensor(out=m1, in0=acc4, in1=cos4, op=ALU.mult)
            nc.vector.tensor_tensor(out=m2, in0=acc4[:, :, :, ::-1], in1=sin4, op=ALU.mult)

        def products5(acc5, m1, m2, cos5, sin5):
            nc.vector.tensor_tensor(out=m1, in0=acc5, in1=cos5, op=ALU.mult)
            nc.vector.tensor_tensor(out=m2, in0=acc5[:, :, :, :, ::-1], in1=sin5, op=ALU.mult)

        def rope(bank):
            acc = acc_of[bank]
            if bank[0] == "Q":
                s, b, jb = bank[1:]
                c, col0, width = PIECES[s]
                nh = width // HD
                tpb = CH // width
                half = jb % 2
                if half == 0:
                    m1 = prod_pool.tile([P, nh, 2 * tpb, HD], F32)
                    m2 = prod_pool.tile([P, nh, 2 * tpb, HD], F32)
                    prod_of[(s, b)] = (m1, m2)
                m1, m2 = prod_of[(s, b)]
                j0 = jb * tpb
                if tpb == 1:
                    products(
                        acc[:, 0, :].rearrange("p (h k e) -> p h k e", h=nh, e=2),
                        m1[:, :, half, :].rearrange("p h (k e) -> p h k e", e=2),
                        m2[:, :, half, :].rearrange("p h (k e) -> p h k e", e=2),
                        cos_t[:, j0 : j0 + 1].to_broadcast([P, nh, NK, 2]),
                        sin_t[:, j0 : j0 + 1].to_broadcast([P, nh, NK, 2]),
                    )
                else:
                    mine = slice(half * tpb, (half + 1) * tpb)
                    products5(
                        acc[:].rearrange("p a (h k e) -> p a h k e", h=nh, e=2),
                        m1[:, :, mine, :].rearrange("p h a (k e) -> p a h k e", e=2),
                        m2[:, :, mine, :].rearrange("p h a (k e) -> p a h k e", e=2),
                        cos_t[:, j0 : j0 + tpb].unsqueeze(2).to_broadcast([P, tpb, nh, NK, 2]),
                        sin_t[:, j0 : j0 + tpb].unsqueeze(2).to_broadcast([P, tpb, nh, NK, 2]),
                    )
                if half == 1:
                    head0 = (c * CH + col0) // HD
                    nc.gpsimd.tensor_tensor(out=m1[:], in0=m1[:], in1=m2[:], op=ALU.add)
                    nc.sync.dma_start(
                        out=out_0[b, head0 : head0 + nh].rearrange("h (p j) d -> p h (j d)", j=JT)[
                            :, :, (j0 - tpb) * HD : (j0 + tpb) * HD
                        ],
                        in_=m1[:].rearrange("p h a d -> p h (a d)"),
                    )
            else:
                b, jh = bank[1:]
                if jh == 0:
                    km1 = kv_pool.tile([P, JT, HD], F32)
                    km2 = kv_pool.tile([P, JT, HD], F32)
                    vo = kv_pool.tile([P, JT, HD], F32)
                    prod_of[("K", b)] = (km1, km2, vo)
                km1, km2, vo = prod_of[("K", b)]
                js = slice(2 * jh, 2 * jh + 2)
                nc.scalar.copy(out=vo[:, js, :], in_=acc[:, :, HD : 2 * HD])
                products(
                    acc[:, :, 0:HD].rearrange("p a (k e) -> p a k e", e=2),
                    km1[:, js, :].rearrange("p a (k e) -> p a k e", e=2),
                    km2[:, js, :].rearrange("p a (k e) -> p a k e", e=2),
                    cos_t[:, js],
                    sin_t[:, js],
                )
                if jh == 1:
                    nc.sync.dma_start(
                        out=out_2[b].rearrange("(p j) d -> p (j d)", j=JT), in_=vo[:].rearrange("p j d -> p (j d)")
                    )
                if b == B - 1:
                    nc.vector.tensor_tensor(out=km1[:, js, :], in0=km1[:, js, :], in1=km2[:, js, :], op=ALU.add)
                    nc.sync.dma_start(
                        out=out_1[b].rearrange("(p j) d -> p j d", j=JT)[:, js, :].rearrange("p j d -> p (j d)"),
                        in_=km1[:, js, :].rearrange("p j d -> p (j d)"),
                    )
                elif jh == 1:
                    nc.gpsimd.tensor_tensor(out=km1[:], in0=km1[:], in1=km2[:], op=ALU.add)
                    nc.sync.dma_start(
                        out=out_1[b].rearrange("(p j) d -> p (j d)", j=JT), in_=km1[:].rearrange("p j d -> p (j d)")
                    )

        tables_angles()
        new_group(0)
        widen(0, 0, "VVVV")
        widen(0, 1, "SSVV")
        for i in range(X_FIRST):
            x_transposes(i)
            if i % 2 == 1:
                keep_clock(WARM_BETWEEN)
        x_copy(0)
        x_copy(1)
        inter(0, 0, "V")
        inter(0, 1, "V")
        quant_w(0)
        x_quant(0, 2)
        tables_sines()
        tables_finish()
        x_copy(2)
        x_copy(3)
        x_quant(2, 2)
        for i in range(JT, X_FIRST):
            x_copy(i)
        new_group(1)
        widen(1, 0, "SSSS")
        for n in range(AHEAD):
            matmuls(banks[n])
        for i in range(X_FIRST, B * JT):
            x_transposes(i)
            x_copy(i)
        inter(1, 0, "S")
        widen(1, 1, "SSSS")
        inter(1, 1, "S")
        for n in range(len(banks)):
            if n == 2:
                x_quant(JT, JT)
            if n + AHEAD in first_bank[1:]:
                s = first_bank.index(n + AHEAD)
                quant_w(s)
                if s + 1 < len(PIECES):
                    prep_on_scalar(s + 1)
                else:
                    kv_inter()
            if n == NCH * B * JT - AHEAD:
                kv_quant()
            if n + AHEAD < len(banks):
                matmuls(banks[n + AHEAD])
            rope(banks[n])
